import numpy as np
import ml_dtypes


def mxq(x, axis, fmt="e4m3"):
    dtype, down = {"e4m3": (ml_dtypes.float8_e4m3fn, 7), "e5m2": (ml_dtypes.float8_e5m2, 14)}[fmt]
    v = np.moveaxis(np.asarray(x, np.float32).astype(ml_dtypes.bfloat16).astype(np.float64), axis, -1)
    blocks = v.reshape(v.shape[:-1] + (-1, 32))
    amax = np.abs(blocks).max(-1, keepdims=True)
    byte = np.maximum(np.where(amax > 0, np.frexp(amax)[1] - 1 + 127, 0) - down, 1)
    scale = np.exp2(byte - 127.0)
    codes = (blocks / scale).astype(np.float32).astype(dtype).astype(np.float64)
    return np.moveaxis((codes * scale).reshape(v.shape), -1, axis)


WIDE = False


def mx_kscale(k):
    if not WIDE:
        return np.ones(k)
    levels = np.array([10, -10, 5, -5, 0])
    if k % 512:
        return np.exp2(np.random.permutation(np.resize(levels, k // 32))).repeat(32)
    a = np.empty((k // 512, 16))
    for p in range(k // 512):
        a[p, :8] = np.random.permutation(np.resize(levels, 8))
        for g in range(8):
            far = levels[np.abs(levels - a[p, g]) >= 10]
            a[p, g + 8] = far[np.random.randint(len(far))]
    return np.exp2(a.ravel()).repeat(32)


BF16 = ml_dtypes.bfloat16


def bf(x):
    return np.asarray(x, np.float32).astype(BF16)


def f64(x):
    return np.asarray(x).astype(np.float64)


B, In, H, Hh, E, G = 512, 1024, 1024, 256, 128, 4
K = In + H
EPS = 1e-6


def rn(*shape):
    return np.random.standard_normal(shape)


def sigmoid(v):
    return 1.0 / (1.0 + np.exp(-v))


def ln(a, gamma, beta):
    mean = a.mean(-1, keepdims=True)
    std = a.std(-1, keepdims=True, ddof=1)
    return gamma * (a - mean) / (std + EPS) + beta


def setup_inputs():
    s = mx_kscale(K)
    return {
        'x': bf(rn(B, In) * s[:In]),
        'h': bf(rn(B, H) * s[In:]),
        'hyper_h': bf(rn(B, Hh)),
        'hyper_c': bf(rn(B, Hh)),
        'hc_Wih': bf(rn(G * Hh, K) / np.sqrt(K) / s[None, :]),
        'hc_bih': bf(0.3 * rn(G * Hh)),
        'hc_Whh': bf(rn(G * Hh, Hh) / np.sqrt(Hh)),
        'hc_ln_gamma': bf(1.0 + 0.1 * rn(G, Hh)),
        'hc_ln_beta': bf(0.1 * rn(G, Hh)),
        'hc_lnc_gamma': bf(1.0 + 0.1 * rn(Hh)),
        'hc_lnc_beta': bf(0.1 * rn(Hh)),
    }


def reference(x, h, hyper_h, hyper_c, hc_Wih, hc_bih, hc_Whh, hc_ln_gamma, hc_ln_beta, hc_lnc_gamma, hc_lnc_beta):
    hyper_in = np.concatenate([f64(x), f64(h)], axis=1)
    v = (mxq(hyper_in, 1, 'e4m3') @ mxq(f64(hc_Wih).T, 0, 'e4m3')) + f64(hc_bih) + f64(hyper_h) @ f64(hc_Whh).T
    v = ln(v.reshape(B, G, Hh), f64(hc_ln_gamma), f64(hc_ln_beta))
    hi, hf, hg, ho = v[:, 0], v[:, 1], v[:, 2], v[:, 3]
    hf = hf + 1.0
    new_hyper_c = f64(hyper_c) * sigmoid(hf) + sigmoid(hi) * np.tanh(hg)
    new_hyper_c = ln(new_hyper_c, f64(hc_lnc_gamma), f64(hc_lnc_beta))
    new_hyper_h = np.tanh(new_hyper_c) * sigmoid(ho)
    return new_hyper_h, new_hyper_c

@@ -1,0 +1,500 @@
+import math
+from contextlib import ExitStack
+
+import concourse.mybir as mybir
+from concourse.masks import make_identity
+
+F32 = mybir.dt.float32
+BF16 = mybir.dt.bfloat16
+U32 = mybir.dt.uint32
+U8 = mybir.dt.uint8
+FP8X4 = mybir.dt.float8_e4m3fn_x4
+ALU = mybir.AluOpType
+ACT = mybir.ActivationFunctionType
+
+P = 128
+BATCH = 512
+BT = BATCH // P
+IN = 1024
+K = 2 * IN
+UNITS = 256
+GATES = 4
+N = GATES * UNITS
+KH = UNITS // P
+K_PASS = 4 * P
+PASSES = K // K_PASS
+PASS_WORDS = K_PASS // 2
+BANK = 512
+EPS = 1e-6
+
+FLOPS = 2 * BATCH * N * K + 2 * BATCH * N * UNITS
+
+
+def tile_hyperlstmcell_pa_kernel(
+    tc,
+    x,
+    h,
+    hyper_h,
+    hyper_c,
+    hc_Wih,
+    hc_bih,
+    hc_Whh,
+    hc_ln_gamma,
+    hc_ln_beta,
+    hc_lnc_gamma,
+    hc_lnc_beta,
+    out_0,
+    out_1,
+):
+    nc = tc.nc
+    with ExitStack() as stack:
+        stack.enter_context(tc.manual_schedule())
+        consts = stack.enter_context(tc.tile_pool(name="consts", bufs=1))
+        raw = stack.enter_context(tc.tile_pool(name="raw", bufs=1))
+        operands = stack.enter_context(tc.tile_pool(name="operands", bufs=1))
+        stage = stack.enter_context(tc.tile_pool(name="stage", bufs=4))
+        work = stack.enter_context(tc.tile_pool(name="work", bufs=2))
+        small = stack.enter_context(tc.tile_pool(name="small", bufs=3))
+        keep = stack.enter_context(tc.tile_pool(name="keep", bufs=1))
+        flip_psum = stack.enter_context(tc.psum_pool(name="flip_psum", bufs=4))
+        mx_psum = stack.enter_context(tc.psum_pool(name="mx_psum", bufs=2))
+        plain_psum = stack.enter_context(tc.psum_pool(name="plain_psum", bufs=2))
+
+        def block(t):
+            return slice(t * UNITS, (t + 1) * UNITS)
+
+        norm_rows = consts.tile([P, P], BF16)
+        nc.vector.memset(norm_rows[:], 0.0)
+        bias_row = consts.tile([P, N], BF16)
+        nc.vector.memset(bias_row[:], 0.0)
+        ones = consts.tile([P, P], BF16)
+        nc.vector.memset(ones[:], 1.0)
+        half_power = consts.tile([P, BT], F32)
+        nc.vector.memset(half_power[:], 0.5)
+        one_column = consts.tile([P, 1], F32)
+        nc.vector.memset(one_column[:], 1.0)
+        ident_bf16 = consts.tile([P, P], BF16)
+        make_identity(nc, ident_bf16[:])
+        ident_f32 = consts.tile([P, P], F32)
+        make_identity(nc, ident_f32[:])
+        table_warmer = consts.tile([P, 1], F32)
+        nc.scalar.activation(out=table_warmer[:], in_=one_column[:], func=ACT.Sigmoid)
+
+        hh_raw = raw.tile([P, BT * UNITS], BF16)
+        nc.sync.dma_start(out=hh_raw[:], in_=hyper_h.rearrange("(p t) k -> p (t k)", t=BT))
+        nc.sync.dma_start(out=norm_rows[0:8, :], in_=hc_ln_gamma.rearrange("g (c q) -> (g c) q", q=P))
+        nc.sync.dma_start(out=norm_rows[8:16, :], in_=hc_ln_beta.rearrange("g (c q) -> (g c) q", q=P))
+        nc.sync.dma_start(out=norm_rows[16:18, :], in_=hc_lnc_gamma.rearrange("(c q) -> c q", q=P))
+        nc.sync.dma_start(out=norm_rows[18:20, :], in_=hc_lnc_beta.rearrange("(c q) -> c q", q=P))
+        nc.sync.dma_start(out=bias_row[0:1, :], in_=hc_bih.rearrange("(o n) -> o n", o=1))
+        whh_raw = raw.tile([P, (N // P) * UNITS], BF16)
+        nc.sync.dma_start(
+            out=whh_raw[:].rearrange("p (j k) -> p j k", k=UNITS),
+            in_=hc_Whh.rearrange("(j p) k -> p j k", p=P),
+        )
+        x_raw = raw.tile([P, BT * IN], BF16)
+        nc.sync.dma_start(out=x_raw[:], in_=x.rearrange("(p t) k -> p (t k)", t=BT))
+        h_raw = raw.tile([P, BT * IN], BF16)
+        nc.sync.dma_start(out=h_raw[:], in_=h.rearrange("(p t) k -> p (t k)", t=BT))
+        c_raw = raw.tile([P, BT * UNITS], BF16)
+        w_raw = []
+        for gate in range(GATES):
+            w_gate = raw.tile([P, 2 * K], BF16, name="w_raw%d" % gate)
+            nc.sync.dma_start(
+                out=w_gate[:].rearrange("p (j k) -> p j k", k=K),
+                in_=hc_Wih[gate * UNITS : (gate + 1) * UNITS, :].rearrange("(j p) k -> p j k", p=P),
+            )
+            w_raw.append(w_gate)
+            if gate == 1:
+                nc.sync.dma_start(out=c_raw[:], in_=hyper_c.rearrange("(p t) n -> p (t n)", t=BT))
+
+        hh_t = operands.tile([P, KH * BT * P], BF16)
+        hh_t_psum = flip_psum.tile([P, 2 * BANK], BF16, tag="flip")
+        for step in range(KH):
+            for t in range(BT):
+                nc.tensor.transpose(
+                    out=hh_t_psum[:, (step * BT + t) * P : (step * BT + t + 1) * P],
+                    in_=hh_raw[:, t * UNITS + step * P : t * UNITS + (step + 1) * P],
+                    identity=ident_bf16[:],
+                )
+        nc.vector.tensor_copy(out=hh_t[:], in_=hh_t_psum[:])
+
+        norm_cols_psum = flip_psum.tile([P, 2 * BANK], BF16, tag="flip")
+        nc.tensor.transpose(out=norm_cols_psum[:, 0:P], in_=norm_rows[:], identity=ident_bf16[:])
+        norm_cols = consts.tile([P, P], BF16)
+        nc.vector.tensor_copy(out=norm_cols[:], in_=norm_cols_psum[:, 0:P])
+        norm_cols_f32 = consts.tile([P, P], F32)
+        nc.vector.tensor_copy(out=norm_cols_f32[:], in_=norm_cols_psum[:, 0:P])
+        GAMMA_CHUNK = 0
+        BETA_CHUNK = N // P
+        LNC_GAMMA_CHUNK = 2 * N // P
+        LNC_BETA_CHUNK = 2 * N // P + UNITS // P
+        GATE_CHUNKS = UNITS // P
+
+        def spread_chunks(bank, first, chunks):
+            for i in range(chunks):
+                nc.tensor.transpose(
+                    out=bank[:, i * P : (i + 1) * P],
+                    in_=norm_cols[:, first + i : first + i + 1].to_broadcast([P, P]),
+                    identity=ident_bf16[:],
+                )
+
+        VECTOR_GATES = 2
+        spread = flip_psum.tile([P, 2 * BANK], BF16, tag="flip")
+        spread_chunks(spread[:, 0 : VECTOR_GATES * UNITS], GAMMA_CHUNK, VECTOR_GATES * GATE_CHUNKS)
+        spread_chunks(spread[:, VECTOR_GATES * UNITS :], BETA_CHUNK, VECTOR_GATES * GATE_CHUNKS)
+        ln_vectors = consts.tile([P, 2 * VECTOR_GATES * UNITS], BF16)
+        nc.vector.tensor_copy(out=ln_vectors[:], in_=spread[:])
+        ln_gamma = ln_vectors[:, 0 : VECTOR_GATES * UNITS]
+        ln_beta = ln_vectors[:, VECTOR_GATES * UNITS :]
+
+        whh_t = operands.tile([P, KH * N], BF16)
+        for step in range(KH):
+            whh_t_psum = flip_psum.tile([P, 2 * BANK], BF16, tag="flip")
+            for j in range(N // P):
+                nc.tensor.transpose(
+                    out=whh_t_psum[:, j * P : (j + 1) * P],
+                    in_=whh_raw[:, j * UNITS + step * P : j * UNITS + (step + 1) * P],
+                    identity=ident_bf16[:],
+                )
+            if step == 0:
+                nc.vector.tensor_copy(out=whh_t[:, step * N : (step + 1) * N], in_=whh_t_psum[:])
+            else:
+                nc.scalar.copy(out=whh_t[:, step * N : (step + 1) * N], in_=whh_t_psum[:])
+
+        plain = operands.tile([P, GATES * BT * UNITS], F32)
+
+        def plain_product(gate):
+            units = slice(gate * UNITS, (gate + 1) * UNITS)
+            for pair in range(BT // 2):
+                bank = plain_psum.tile([P, BANK], F32, tag="plain")
+                for i in range(2):
+                    t = 2 * pair + i
+                    group = bank[:, i * UNITS : (i + 1) * UNITS]
+                    for step in range(KH):
+                        nc.tensor.matmul(
+                            out=group,
+                            lhsT=hh_t[:, (step * BT + t) * P : (step * BT + t + 1) * P],
+                            rhs=whh_t[:, step * N + gate * UNITS : step * N + (gate + 1) * UNITS],
+                            start=(step == 0),
+                            stop=False,
+                        )
+                    nc.tensor.matmul(out=group, lhsT=ones[:], rhs=bias_row[:, units], start=False, stop=True)
+                first = (gate * BT + 2 * pair) * UNITS
+                nc.scalar.copy(out=plain[:, first : first + BANK], in_=bank[:])
+
+        u_codes = operands.tile([P, PASSES * BATCH], U32, align_bytes=64)
+        u_scales = operands.tile([P, PASSES * BATCH], U8, align_bytes=64)
+        w_codes = operands.tile([P, GATES * PASSES * UNITS], U32, align_bytes=64)
+        w_scales = operands.tile([P, GATES * PASSES * UNITS], U8, align_bytes=64)
+
+        def flip(pieces, vector_helps):
+            grouped = stage.tile([P, 2 * BANK * 2], BF16, align_bytes=64, tag="grouped")
+            grouped_words = grouped[:].bitcast(F32)
+            for b in range(2):
+                row_tiles, first_word = pieces[b]
+                bank = flip_psum.tile([P, BANK], F32, tag="flip")
+                for half in range(2):
+                    for i in range(2):
+                        nc.tensor.transpose(
+                            out=bank[:, (2 * half + i) * P : (2 * half + i + 1) * P],
+                            in_=row_tiles[i][:, first_word + half : first_word + PASS_WORDS : 2],
+                            identity=ident_f32[:],
+                        )
+                side_by_side = grouped_words[:, b * BANK : (b + 1) * BANK].rearrange("p (r u) -> p r u", u=2)
+                halves = bank[:].rearrange("p (u r) -> p r u", u=2)
+                if vector_helps and b == 0:
+                    nc.vector.tensor_copy(out=side_by_side, in_=halves)
+                else:
+                    nc.scalar.copy(out=side_by_side, in_=halves)
+            return grouped
+
+        def flip_u(g):
+            source = (x_raw if g < PASSES // 2 else h_raw)[:].bitcast(F32)
+            row_words = IN // 2
+            first_word = (g % (PASSES // 2)) * PASS_WORDS
+            tiles = [source[:, t * row_words : (t + 1) * row_words] for t in range(BT)]
+            return flip([(tiles[0:2], first_word), (tiles[2:4], first_word)], vector_helps=True)
+
+        def quantise_u(g, grouped):
+            cols = slice(g * BATCH, (g + 1) * BATCH)
+            nc.vector.quantize_mx(out=u_codes[:, cols].bitcast(FP8X4), scales=u_scales[:, cols], in_=grouped[:])
+
+        def flip_w(gate, vector_helps):
+            source = w_raw[gate][:].bitcast(F32)
+            row_words = K // 2
+            tiles = [source[:, j * row_words : (j + 1) * row_words] for j in range(2)]
+            return [
+                flip([(tiles, g * PASS_WORDS), (tiles, (g + 1) * PASS_WORDS)], vector_helps)
+                for g in range(0, PASSES, 2)
+            ]
+
+        def quantise_w(gate, i, grouped):
+            first = (gate * PASSES + 2 * i) * UNITS
+            cols = slice(first, first + 2 * UNITS)
+            nc.vector.quantize_mx(out=w_codes[:, cols].bitcast(FP8X4), scales=w_scales[:, cols], in_=grouped[:])
+
+        def negated_mean(sums):
+            neg_mean = small.tile([P, BT], F32, tag="neg_mean")
+            nc.vector.tensor_scalar_mul(out=neg_mean[:], in0=sums[:], scalar1=-1.0 / UNITS)
+            return neg_mean
+
+        def sum_of_squares(values, neg_mean, squares, sum_squares, t):
+            nc.scalar.activation(
+                out=squares[:, block(t)],
+                in_=values[:, block(t)],
+                func=ACT.Square,
+                bias=neg_mean[:, t : t + 1],
+                accum_out=sum_squares[:, t : t + 1],
+            )
+
+        def square_root(sum_squares):
+            root = small.tile([P, BT], F32, tag="root")
+            nc.gpsimd.tensor_tensor(out=root[:], in0=sum_squares[:], in1=half_power[:], op=ALU.pow)
+            return root
+
+        def root_of_squares(values, neg_mean):
+            sum_squares = small.tile([P, BT], F32, tag="sum_squares")
+            squares = work.tile([P, BT * UNITS], F32, tag="squares")
+            for t in range(BT):
+                sum_of_squares(values, neg_mean, squares, sum_squares, t)
+            return square_root(sum_squares)
+
+        def centre(values, neg_mean, gamma):
+            centred = work.tile([P, BT * UNITS], F32, tag="centred")
+            for t in range(BT):
+                nc.vector.scalar_tensor_tensor(
+                    out=centred[:, block(t)],
+                    in0=values[:, block(t)],
+                    scalar=neg_mean[:, t : t + 1],
+                    in1=gamma,
+                    op0=ALU.add,
+                    op1=ALU.mult,
+                )
+            return centred
+
+        def std_plus_eps(root):
+            std_eps = small.tile([P, BT], F32, tag="std_eps")
+            nc.vector.tensor_scalar(
+                out=std_eps[:],
+                in0=root[:],
+                scalar1=1.0 / math.sqrt(UNITS - 1),
+                scalar2=EPS,
+                op0=ALU.mult,
+                op1=ALU.add,
+            )
+            return std_eps
+
+        def inverse(std_eps):
+            inv_std = small.tile([P, BT], F32, tag="inv_std")
+            nc.vector.reciprocal(out=inv_std[:], in_=std_eps[:])
+            return inv_std
+
+        def scale_and_shift(centred, inv_std, beta, out):
+            for t in range(BT):
+                nc.vector.scalar_tensor_tensor(
+                    out=out[:, block(t)],
+                    in0=centred[:, block(t)],
+                    scalar=inv_std[:, t : t + 1],
+                    in1=beta,
+                    op0=ALU.mult,
+                    op1=ALU.add,
+                )
+
+        def gate_sums(gate):
+            v = work.tile([P, BT * UNITS], F32, tag="v")
+            v_sums = small.tile([P, BT], F32, tag="v_sums")
+            for pair in range(BT // 2):
+                bank = mx_psum.tile([P, BANK], F32, tag="mx")
+                for i in range(2):
+                    t = 2 * pair + i
+                    for g in range(PASSES):
+                        u_cols = slice(g * BATCH + t * P, g * BATCH + (t + 1) * P)
+                        w_cols = slice((gate * PASSES + g) * UNITS, (gate * PASSES + g + 1) * UNITS)
+                        nc.tensor.matmul_mx(
+                            out=bank[:, i * UNITS : (i + 1) * UNITS],
+                            lhsT=u_codes[:, u_cols].bitcast(FP8X4),
+                            lhsT_scale=u_scales[:, u_cols],
+                            rhs=w_codes[:, w_cols].bitcast(FP8X4),
+                            rhs_scale=w_scales[:, w_cols],
+                            start=(g == 0),
+                            stop=(g == PASSES - 1),
+                        )
+                for i in range(2):
+                    t = 2 * pair + i
+                    nc.vector.scalar_tensor_tensor(
+                        out=v[:, block(t)],
+                        in0=bank[:, i * UNITS : (i + 1) * UNITS],
+                        scalar=1.0,
+                        in1=plain[:, (gate * BT + t) * UNITS : (gate * BT + t + 1) * UNITS],
+                        op0=ALU.mult,
+                        op1=ALU.add,
+                        accum_out=v_sums[:, t : t + 1],
+                    )
+            return v, v_sums
+
+        def gate_cols(gate):
+            return slice(gate * UNITS, (gate + 1) * UNITS)
+
+        gates = [keep.tile([P, BT * UNITS], F32, name="gate%d" % gate) for gate in range(VECTOR_GATES)]
+
+        def activate(gate, normed):
+            if gate == 1:
+                nc.scalar.activation(out=gates[gate][:], in_=normed[:], func=ACT.Sigmoid, bias=one_column[:])
+            else:
+                nc.scalar.activation(out=gates[gate][:], in_=normed[:], func=ACT.Sigmoid)
+
+        def row_scale_and_bias(neg_mean, root):
+            inv_std = inverse(std_plus_eps(root))
+            neg_mean_over_std = small.tile([P, BT], F32, tag="neg_mean_over_std")
+            nc.vector.tensor_tensor(out=neg_mean_over_std[:], in0=neg_mean[:], in1=inv_std[:], op=ALU.mult)
+            return inv_std, neg_mean_over_std
+
+        def gate_by_transposes(gate, func, v, inv_std, neg_mean_over_std, result_psum, result_tag):
+            normed = work.tile([P, BT * UNITS], F32, tag="normed")
+            flipped = []
+            for pair in range(BT // 2):
+                bank = flip_psum.tile([P, BANK], F32, tag="flip")
+                for i in range(2):
+                    t = 2 * pair + i
+                    nc.scalar.activation(
+                        out=normed[:, block(t)],
+                        in_=v[:, block(t)],
+                        func=ACT.Identity,
+                        scale=inv_std[:, t : t + 1],
+                        bias=neg_mean_over_std[:, t : t + 1],
+                    )
+                for c in range(GATE_CHUNKS):
+                    for i in range(2):
+                        t = 2 * pair + i
+                        nc.tensor.transpose(
+                            out=bank[:, (2 * c + i) * P : (2 * c + i + 1) * P],
+                            in_=normed[:, t * UNITS + c * P : t * UNITS + (c + 1) * P],
+                            identity=ident_f32[:],
+                        )
+                flipped.append(bank)
+            gate_t = work.tile([P, BT * UNITS], F32, tag="gate_t")
+            result = []
+            for pair in range(BT // 2):
+                for c in range(GATE_CHUNKS):
+                    gamma_chunk = GAMMA_CHUNK + gate * GATE_CHUNKS + c
+                    beta_chunk = BETA_CHUNK + gate * GATE_CHUNKS + c
+                    nc.scalar.activation(
+                        out=gate_t[:, (2 * pair + c) * UNITS : (2 * pair + c + 1) * UNITS],
+                        in_=flipped[pair][:, c * UNITS : (c + 1) * UNITS],
+                        func=func,
+                        scale=norm_cols_f32[:, gamma_chunk : gamma_chunk + 1],
+                        bias=norm_cols_f32[:, beta_chunk : beta_chunk + 1],
+                    )
+                bank = result_psum.tile([P, BANK], F32, tag=result_tag)
+                for i in range(2):
+                    for c in range(GATE_CHUNKS):
+                        first = (2 * pair + c) * UNITS + i * P
+                        nc.tensor.transpose(
+                            out=bank[:, i * UNITS + c * P : i * UNITS + (c + 1) * P],
+                            in_=gate_t[:, first : first + P],
+                            identity=ident_f32[:],
+                        )
+                result.append(bank)
+            return result
+
+        grouped_u = [flip_u(0), flip_u(1)]
+        quantise_u(0, grouped_u[0])
+        plain_product(0)
+        quantise_u(1, grouped_u[1])
+        grouped_u = grouped_u + [flip_u(2), flip_u(3)]
+        quantise_u(2, grouped_u[2])
+        quantise_u(3, grouped_u[3])
+        grouped_w = {0: flip_w(0, vector_helps=True)}
+        quantise_w(0, 0, grouped_w[0][0])
+        quantise_w(0, 1, grouped_w[0][1])
+        grouped_w[1] = flip_w(1, vector_helps=False)
+
+        vs = []
+        neg_means = []
+        roots = []
+        centreds = []
+        for gate in range(GATES - 1):
+            before = gate - 1
+            v, v_sums = gate_sums(gate)
+            vs.append(v)
+            neg_means.append(negated_mean(v_sums))
+            roots.append(root_of_squares(v, neg_means[gate]))
+            plain_product(gate + 1)
+            quantise_w(gate + 1, 0, grouped_w[gate + 1][0])
+            if before >= 0:
+                std_eps = std_plus_eps(roots[before])
+            quantise_w(gate + 1, 1, grouped_w[gate + 1][1])
+            if before >= 0:
+                inv_std = inverse(std_eps)
+            if gate < VECTOR_GATES:
+                centreds.append(centre(v, neg_means[gate], ln_gamma[:, gate_cols(gate)]))
+            if before >= 0:
+                normed = work.tile([P, BT * UNITS], F32, tag="normed")
+                scale_and_shift(centreds[before], inv_std, ln_beta[:, gate_cols(before)], normed)
+            if gate + 2 < GATES:
+                grouped_w[gate + 2] = flip_w(gate + 2, vector_helps=False)
+            if before >= 0:
+                activate(before, normed)
+
+        late = flip_psum.tile([P, 2 * BANK], BF16, tag="flip")
+        spread_chunks(late[:, 0:UNITS], LNC_GAMMA_CHUNK, GATE_CHUNKS)
+        spread_chunks(late[:, UNITS : 2 * UNITS], LNC_BETA_CHUNK, GATE_CHUNKS)
+        lnc_gamma = late[:, 0:UNITS]
+        lnc_beta = late[:, UNITS : 2 * UNITS]
+
+        inv_std, neg_mean_over_std = row_scale_and_bias(neg_means[2], roots[2])
+        v, v_sums = gate_sums(3)
+        gate_g = gate_by_transposes(2, ACT.Tanh, vs[2], inv_std, neg_mean_over_std, mx_psum, "mx")
+        neg_mean = negated_mean(v_sums)
+        kept = keep.tile([P, BT * UNITS], F32)
+        nc.vector.tensor_tensor(out=kept[:], in0=gates[1][:], in1=c_raw[:], op=ALU.mult)
+        root = root_of_squares(v, neg_mean)
+
+        fresh = keep.tile([P, BT * UNITS], F32)
+        for pair in range(BT // 2):
+            cols = slice(pair * BANK, (pair + 1) * BANK)
+            nc.vector.tensor_tensor(out=fresh[:, cols], in0=gates[0][:, cols], in1=gate_g[pair][:], op=ALU.mult)
+        cell = keep.tile([P, BT * UNITS], F32)
+        cell_sums = small.tile([P, BT], F32)
+        cell_neg_mean = small.tile([P, BT], F32)
+        cell_sum_squares = small.tile([P, BT], F32)
+        squares = work.tile([P, BT * UNITS], F32, tag="squares")
+        for t in range(BT + 1):
+            if t < BT:
+                nc.vector.scalar_tensor_tensor(
+                    out=cell[:, block(t)],
+                    in0=kept[:, block(t)],
+                    scalar=1.0,
+                    in1=fresh[:, block(t)],
+                    op0=ALU.mult,
+                    op1=ALU.add,
+                    accum_out=cell_sums[:, t : t + 1],
+                )
+            if t >= 1:
+                done = slice(t - 1, t)
+                nc.vector.tensor_scalar_mul(out=cell_neg_mean[:, done], in0=cell_sums[:, done], scalar1=-1.0 / UNITS)
+                sum_of_squares(cell, cell_neg_mean, squares, cell_sum_squares, t - 1)
+        cell_root = square_root(cell_sum_squares)
+
+        inv_std, neg_mean_over_std = row_scale_and_bias(neg_mean, root)
+        gate_o = gate_by_transposes(3, ACT.Sigmoid, v, inv_std, neg_mean_over_std, plain_psum, "plain")
+
+        cell_centred = centre(cell, cell_neg_mean, lnc_gamma)
+        new_c = keep.tile([P, BT * UNITS], F32)
+        scale_and_shift(cell_centred, inverse(std_plus_eps(cell_root)), lnc_beta, new_c)
+        out_0_tiles = out_0.rearrange("(p t) n -> p t n", t=BT)
+        out_1_tiles = out_1.rearrange("(p t) n -> p t n", t=BT)
+        for t in range(BT):
+            nc.sync.dma_start(out=out_1_tiles[:, t, :], in_=new_c[:, block(t)])
+        tanh_c = keep.tile([P, BT * UNITS], F32)
+        new_h = keep.tile([P, BT * UNITS], F32)
+        for t in range(BT):
+            nc.scalar.activation(out=tanh_c[:, block(t)], in_=new_c[:, block(t)], func=ACT.Tanh)
+            nc.vector.tensor_tensor(
+                out=new_h[:, block(t)],
+                in0=tanh_c[:, block(t)],
+                in1=gate_o[t // 2][:, (t % 2) * UNITS : (t % 2 + 1) * UNITS],
+                op=ALU.mult,
+            )
+            nc.sync.dma_start(out=out_0_tiles[:, t, :], in_=new_h[:, block(t)])

@@ -54,7 +54,7 @@ def tile_hyperlstmcell_pa_kernel(
         operands = stack.enter_context(tc.tile_pool(name="operands", bufs=1))
         stage = stack.enter_context(tc.tile_pool(name="stage", bufs=4))
         work = stack.enter_context(tc.tile_pool(name="work", bufs=2))
-        small = stack.enter_context(tc.tile_pool(name="small", bufs=3))
+        small = stack.enter_context(tc.tile_pool(name="small", bufs=1))
         keep = stack.enter_context(tc.tile_pool(name="keep", bufs=1))
         flip_psum = stack.enter_context(tc.psum_pool(name="flip_psum", bufs=4))
         mx_psum = stack.enter_context(tc.psum_pool(name="mx_psum", bufs=2))
@@ -65,10 +65,6 @@ def tile_hyperlstmcell_pa_kernel(
 
         norm_rows = consts.tile([P, P], BF16)
         nc.vector.memset(norm_rows[:], 0.0)
-        bias_row = consts.tile([P, N], BF16)
-        nc.vector.memset(bias_row[:], 0.0)
-        ones = consts.tile([P, P], BF16)
-        nc.vector.memset(ones[:], 1.0)
         half_power = consts.tile([P, BT], F32)
         nc.vector.memset(half_power[:], 0.5)
         one_column = consts.tile([P, 1], F32)
@@ -80,21 +76,38 @@ def tile_hyperlstmcell_pa_kernel(
         table_warmer = consts.tile([P, 1], F32)
         nc.scalar.activation(out=table_warmer[:], in_=one_column[:], func=ACT.Sigmoid)
 
+        GATE_CHUNKS = UNITS // P
+        BIAS_CHUNK = 0
+        GAMMA_CHUNK = BIAS_CHUNK + N // P
+        BETA_CHUNK = GAMMA_CHUNK + N // P
+        LNC_GAMMA_CHUNK = BETA_CHUNK + N // P
+        LNC_BETA_CHUNK = LNC_GAMMA_CHUNK + GATE_CHUNKS
+
+        x_raw = raw.tile([P, BT * IN], BF16)
+        h_raw = raw.tile([P, BT * IN], BF16)
+        half_cols = (slice(0, BT // 2 * IN), slice(BT // 2 * IN, BT * IN))
+        x_rows = x.rearrange("(p t) k -> p (t k)", t=BT)
+        for cols in half_cols:
+            nc.sync.dma_start(out=x_raw[:, cols], in_=x_rows[:, cols])
         hh_raw = raw.tile([P, BT * UNITS], BF16)
         nc.sync.dma_start(out=hh_raw[:], in_=hyper_h.rearrange("(p t) k -> p (t k)", t=BT))
-        nc.sync.dma_start(out=norm_rows[0:8, :], in_=hc_ln_gamma.rearrange("g (c q) -> (g c) q", q=P))
-        nc.sync.dma_start(out=norm_rows[8:16, :], in_=hc_ln_beta.rearrange("g (c q) -> (g c) q", q=P))
-        nc.sync.dma_start(out=norm_rows[16:18, :], in_=hc_lnc_gamma.rearrange("(c q) -> c q", q=P))
-        nc.sync.dma_start(out=norm_rows[18:20, :], in_=hc_lnc_beta.rearrange("(c q) -> c q", q=P))
-        nc.sync.dma_start(out=bias_row[0:1, :], in_=hc_bih.rearrange("(o n) -> o n", o=1))
+        nc.sync.dma_start(out=norm_rows[BIAS_CHUNK:GAMMA_CHUNK, :], in_=hc_bih.rearrange("(c q) -> c q", q=P))
+        nc.sync.dma_start(out=norm_rows[GAMMA_CHUNK:BETA_CHUNK, :], in_=hc_ln_gamma.rearrange("g (c q) -> (g c) q", q=P))
+        nc.sync.dma_start(
+            out=norm_rows[BETA_CHUNK:LNC_GAMMA_CHUNK, :], in_=hc_ln_beta.rearrange("g (c q) -> (g c) q", q=P)
+        )
+        nc.sync.dma_start(
+            out=norm_rows[LNC_GAMMA_CHUNK:LNC_BETA_CHUNK, :], in_=hc_lnc_gamma.rearrange("(c q) -> c q", q=P)
+        )
+        nc.sync.dma_start(
+            out=norm_rows[LNC_BETA_CHUNK : LNC_BETA_CHUNK + GATE_CHUNKS, :],
+            in_=hc_lnc_beta.rearrange("(c q) -> c q", q=P),
+        )
         whh_raw = raw.tile([P, (N // P) * UNITS], BF16)
         nc.sync.dma_start(
             out=whh_raw[:].rearrange("p (j k) -> p j k", k=UNITS),
             in_=hc_Whh.rearrange("(j p) k -> p j k", p=P),
         )
-        x_raw = raw.tile([P, BT * IN], BF16)
-        nc.sync.dma_start(out=x_raw[:], in_=x.rearrange("(p t) k -> p (t k)", t=BT))
-        h_raw = raw.tile([P, BT * IN], BF16)
         nc.sync.dma_start(out=h_raw[:], in_=h.rearrange("(p t) k -> p (t k)", t=BT))
         c_raw = raw.tile([P, BT * UNITS], BF16)
         w_raw = []
@@ -109,27 +122,41 @@ def tile_hyperlstmcell_pa_kernel(
                 nc.sync.dma_start(out=c_raw[:], in_=hyper_c.rearrange("(p t) n -> p (t n)", t=BT))
 
         hh_t = operands.tile([P, KH * BT * P], BF16)
-        hh_t_psum = flip_psum.tile([P, 2 * BANK], BF16, tag="flip")
-        for step in range(KH):
-            for t in range(BT):
+        whh_t = operands.tile([P, KH * N], BF16)
+
+        def turn_hyper_h():
+            bank = flip_psum.tile([P, 2 * BANK], BF16, tag="flip")
+            for step in range(KH):
+                for t in range(BT):
+                    nc.tensor.transpose(
+                        out=bank[:, (step * BT + t) * P : (step * BT + t + 1) * P],
+                        in_=hh_raw[:, t * UNITS + step * P : t * UNITS + (step + 1) * P],
+                        identity=ident_bf16[:],
+                    )
+            nc.scalar.copy(out=hh_t[:], in_=bank[:])
+
+        def turn_whh(step):
+            bank = flip_psum.tile([P, 2 * BANK], BF16, tag="flip")
+            for j in range(N // P):
                 nc.tensor.transpose(
-                    out=hh_t_psum[:, (step * BT + t) * P : (step * BT + t + 1) * P],
-                    in_=hh_raw[:, t * UNITS + step * P : t * UNITS + (step + 1) * P],
+                    out=bank[:, j * P : (j + 1) * P],
+                    in_=whh_raw[:, j * UNITS + step * P : j * UNITS + (step + 1) * P],
                     identity=ident_bf16[:],
                 )
-        nc.vector.tensor_copy(out=hh_t[:], in_=hh_t_psum[:])
+            nc.scalar.copy(out=whh_t[:, step * N : (step + 1) * N], in_=bank[:])
 
-        norm_cols_psum = flip_psum.tile([P, 2 * BANK], BF16, tag="flip")
-        nc.tensor.transpose(out=norm_cols_psum[:, 0:P], in_=norm_rows[:], identity=ident_bf16[:])
         norm_cols = consts.tile([P, P], BF16)
-        nc.vector.tensor_copy(out=norm_cols[:], in_=norm_cols_psum[:, 0:P])
         norm_cols_f32 = consts.tile([P, P], F32)
-        nc.vector.tensor_copy(out=norm_cols_f32[:], in_=norm_cols_psum[:, 0:P])
-        GAMMA_CHUNK = 0
-        BETA_CHUNK = N // P
-        LNC_GAMMA_CHUNK = 2 * N // P
-        LNC_BETA_CHUNK = 2 * N // P + UNITS // P
-        GATE_CHUNKS = UNITS // P
+        beta_plus_one = consts.tile([P, P], F32)
+
+        def turn_norm_rows():
+            bank = flip_psum.tile([P, 2 * BANK], BF16, tag="flip")
+            nc.tensor.transpose(out=bank[:, 0:P], in_=norm_rows[:], identity=ident_bf16[:])
+            nc.vector.tensor_copy(out=norm_cols[:], in_=bank[:, 0:P])
+            nc.vector.tensor_copy(out=norm_cols_f32[:], in_=bank[:, 0:P])
+            nc.vector.tensor_scalar(
+                out=beta_plus_one[:], in0=bank[:, 0:P], scalar1=1.0, scalar2=1.0, op0=ALU.mult, op1=ALU.add
+            )
 
         def spread_chunks(bank, first, chunks):
             for i in range(chunks):
@@ -139,130 +166,133 @@ def tile_hyperlstmcell_pa_kernel(
                     identity=ident_bf16[:],
                 )
 
-        VECTOR_GATES = 2
-        spread = flip_psum.tile([P, 2 * BANK], BF16, tag="flip")
-        spread_chunks(spread[:, 0 : VECTOR_GATES * UNITS], GAMMA_CHUNK, VECTOR_GATES * GATE_CHUNKS)
-        spread_chunks(spread[:, VECTOR_GATES * UNITS :], BETA_CHUNK, VECTOR_GATES * GATE_CHUNKS)
-        ln_vectors = consts.tile([P, 2 * VECTOR_GATES * UNITS], BF16)
-        nc.vector.tensor_copy(out=ln_vectors[:], in_=spread[:])
-        ln_gamma = ln_vectors[:, 0 : VECTOR_GATES * UNITS]
-        ln_beta = ln_vectors[:, VECTOR_GATES * UNITS :]
+        bias = consts.tile([P, N], BF16)
 
-        whh_t = operands.tile([P, KH * N], BF16)
-        for step in range(KH):
-            whh_t_psum = flip_psum.tile([P, 2 * BANK], BF16, tag="flip")
-            for j in range(N // P):
-                nc.tensor.transpose(
-                    out=whh_t_psum[:, j * P : (j + 1) * P],
-                    in_=whh_raw[:, j * UNITS + step * P : j * UNITS + (step + 1) * P],
-                    identity=ident_bf16[:],
+        def spread_bias():
+            bank = flip_psum.tile([P, 2 * BANK], BF16, tag="flip")
+            spread_chunks(bank[:], BIAS_CHUNK, N // P)
+            nc.vector.tensor_copy(out=bias[:], in_=bank[:])
+
+        CELL_GATE = 2
+        ln_vectors = consts.tile([P, 2 * UNITS], BF16)
+        ln_gamma = ln_vectors[:, 0:UNITS]
+        ln_beta = ln_vectors[:, UNITS : 2 * UNITS]
+
+        def spread_norm_vectors():
+            bank = flip_psum.tile([P, 2 * BANK], BF16, tag="flip")
+            spread_chunks(bank[:, 0:UNITS], GAMMA_CHUNK + CELL_GATE * GATE_CHUNKS, GATE_CHUNKS)
+            spread_chunks(bank[:, UNITS : 2 * UNITS], BETA_CHUNK + CELL_GATE * GATE_CHUNKS, GATE_CHUNKS)
+            nc.vector.tensor_copy(out=ln_vectors[:], in_=bank[:, 0 : 2 * UNITS])
+
+        plain = operands.tile([P, BT * N], F32)
+
+        def plain_product(gate_pair, t):
+            units = slice(gate_pair * BANK, (gate_pair + 1) * BANK)
+            bank = plain_psum.tile([P, BANK], F32, tag="plain")
+            for step in range(KH):
+                nc.tensor.matmul(
+                    out=bank[:],
+                    lhsT=hh_t[:, (step * BT + t) * P : (step * BT + t + 1) * P],
+                    rhs=whh_t[:, step * N + units.start : step * N + units.stop],
+                    start=(step == 0),
+                    stop=(step == KH - 1),
                 )
-            if step == 0:
-                nc.vector.tensor_copy(out=whh_t[:, step * N : (step + 1) * N], in_=whh_t_psum[:])
-            else:
-                nc.scalar.copy(out=whh_t[:, step * N : (step + 1) * N], in_=whh_t_psum[:])
-
-        plain = operands.tile([P, GATES * BT * UNITS], F32)
-
-        def plain_product(gate):
-            units = slice(gate * UNITS, (gate + 1) * UNITS)
-            for pair in range(BT // 2):
-                bank = plain_psum.tile([P, BANK], F32, tag="plain")
-                for i in range(2):
-                    t = 2 * pair + i
-                    group = bank[:, i * UNITS : (i + 1) * UNITS]
-                    for step in range(KH):
-                        nc.tensor.matmul(
-                            out=group,
-                            lhsT=hh_t[:, (step * BT + t) * P : (step * BT + t + 1) * P],
-                            rhs=whh_t[:, step * N + gate * UNITS : step * N + (gate + 1) * UNITS],
-                            start=(step == 0),
-                            stop=False,
-                        )
-                    nc.tensor.matmul(out=group, lhsT=ones[:], rhs=bias_row[:, units], start=False, stop=True)
-                first = (gate * BT + 2 * pair) * UNITS
-                nc.scalar.copy(out=plain[:, first : first + BANK], in_=bank[:])
+            nc.vector.tensor_tensor(
+                out=plain[:, t * N + units.start : t * N + units.stop], in0=bank[:], in1=bias[:, units], op=ALU.add
+            )
 
         u_codes = operands.tile([P, PASSES * BATCH], U32, align_bytes=64)
         u_scales = operands.tile([P, PASSES * BATCH], U8, align_bytes=64)
         w_codes = operands.tile([P, GATES * PASSES * UNITS], U32, align_bytes=64)
         w_scales = operands.tile([P, GATES * PASSES * UNITS], U8, align_bytes=64)
 
-        def flip(pieces, vector_helps):
-            grouped = stage.tile([P, 2 * BANK * 2], BF16, align_bytes=64, tag="grouped")
+        X_WORDS = IN // 2
+        ROW_WORDS = K // 2
+
+        def flip_piece(grouped, b, row_tiles, copy):
             grouped_words = grouped[:].bitcast(F32)
-            for b in range(2):
-                row_tiles, first_word = pieces[b]
-                bank = flip_psum.tile([P, BANK], F32, tag="flip")
-                for half in range(2):
-                    for i in range(2):
-                        nc.tensor.transpose(
-                            out=bank[:, (2 * half + i) * P : (2 * half + i + 1) * P],
-                            in_=row_tiles[i][:, first_word + half : first_word + PASS_WORDS : 2],
-                            identity=ident_f32[:],
-                        )
-                side_by_side = grouped_words[:, b * BANK : (b + 1) * BANK].rearrange("p (r u) -> p r u", u=2)
-                halves = bank[:].rearrange("p (u r) -> p r u", u=2)
-                if vector_helps and b == 0:
-                    nc.vector.tensor_copy(out=side_by_side, in_=halves)
-                else:
-                    nc.scalar.copy(out=side_by_side, in_=halves)
+            bank = flip_psum.tile([P, BANK], F32, tag="flip")
+            for parity in range(2):
+                for i in range(2):
+                    nc.tensor.transpose(
+                        out=bank[:, (2 * parity + i) * P : (2 * parity + i + 1) * P],
+                        in_=row_tiles[i](parity),
+                        identity=ident_f32[:],
+                    )
+            copy(
+                out=grouped_words[:, b * BANK : (b + 1) * BANK].rearrange("p (r u) -> p r u", u=2),
+                in_=bank[:].rearrange("p (u r) -> p r u", u=2),
+            )
+
+        def new_grouped():
+            grouped = stage.tile([P, 2 * BANK * 2], BF16, align_bytes=64, tag="grouped")
             return grouped
 
-        def flip_u(g):
-            source = (x_raw if g < PASSES // 2 else h_raw)[:].bitcast(F32)
-            row_words = IN // 2
-            first_word = (g % (PASSES // 2)) * PASS_WORDS
-            tiles = [source[:, t * row_words : (t + 1) * row_words] for t in range(BT)]
-            return flip([(tiles[0:2], first_word), (tiles[2:4], first_word)], vector_helps=True)
+        def flip_u(g, b, grouped, copy):
+            words = (x_raw if g < PASSES // 2 else h_raw)[:].bitcast(F32)
+            firsts = [t * X_WORDS + (g % (PASSES // 2)) * PASS_WORDS for t in (2 * b, 2 * b + 1)]
+            flip_piece(grouped, b, [every_second(words, first) for first in firsts], copy)
+
+        def every_second(words, first):
+            return lambda parity: words[:, first + parity : first + PASS_WORDS : 2]
+
+        def w_half(gate, j, g):
+            words = w_raw[gate][:].bitcast(F32)
+            first = j * ROW_WORDS + g * PASS_WORDS
+            return lambda parity: words[:, first + parity : first + PASS_WORDS : 2]
+
+        def flip_w(gate, i, b, grouped, copy):
+            flip_piece(grouped, b, [w_half(gate, j, 2 * i + b) for j in range(2)], copy)
 
         def quantise_u(g, grouped):
             cols = slice(g * BATCH, (g + 1) * BATCH)
             nc.vector.quantize_mx(out=u_codes[:, cols].bitcast(FP8X4), scales=u_scales[:, cols], in_=grouped[:])
-
-        def flip_w(gate, vector_helps):
-            source = w_raw[gate][:].bitcast(F32)
-            row_words = K // 2
-            tiles = [source[:, j * row_words : (j + 1) * row_words] for j in range(2)]
-            return [
-                flip([(tiles, g * PASS_WORDS), (tiles, (g + 1) * PASS_WORDS)], vector_helps)
-                for g in range(0, PASSES, 2)
-            ]
 
         def quantise_w(gate, i, grouped):
             first = (gate * PASSES + 2 * i) * UNITS
             cols = slice(first, first + 2 * UNITS)
             nc.vector.quantize_mx(out=w_codes[:, cols].bitcast(FP8X4), scales=w_scales[:, cols], in_=grouped[:])
 
-        def negated_mean(sums):
-            neg_mean = small.tile([P, BT], F32, tag="neg_mean")
-            nc.vector.tensor_scalar_mul(out=neg_mean[:], in0=sums[:], scalar1=-1.0 / UNITS)
-            return neg_mean
+        def cols_of(tiles):
+            return slice(tiles.start, tiles.stop)
 
-        def sum_of_squares(values, neg_mean, squares, sum_squares, t):
-            nc.scalar.activation(
-                out=squares[:, block(t)],
-                in_=values[:, block(t)],
-                func=ACT.Square,
-                bias=neg_mean[:, t : t + 1],
-                accum_out=sum_squares[:, t : t + 1],
+
+        def negated_mean(sums, neg_mean, tiles):
+            cols = cols_of(tiles)
+            nc.vector.tensor_scalar_mul(out=neg_mean[:, cols], in0=sums[:, cols], scalar1=-1.0 / UNITS)
+
+        def sum_of_squares(values, sums, squares, sum_squares, tiles):
+            for t in tiles:
+                nc.scalar.activation(
+                    out=squares[:, block(t)],
+                    in_=values[:, block(t)],
+                    func=ACT.Square,
+                    scale=-float(UNITS),
+                    bias=sums[:, t : t + 1],
+                    accum_out=sum_squares[:, t : t + 1],
+                )
+
+        def square_root(sum_squares, root, tiles):
+            cols = cols_of(tiles)
+            nc.gpsimd.tensor_tensor(out=root[:, cols], in0=sum_squares[:, cols], in1=half_power[:, cols], op=ALU.pow)
+
+        def std_plus_eps(root, std_eps, tiles):
+            cols = cols_of(tiles)
+            nc.vector.tensor_scalar(
+                out=std_eps[:, cols],
+                in0=root[:, cols],
+                scalar1=1.0 / (UNITS * math.sqrt(UNITS - 1)),
+                scalar2=EPS,
+                op0=ALU.mult,
+                op1=ALU.add,
             )
 
-        def square_root(sum_squares):
-            root = small.tile([P, BT], F32, tag="root")
-            nc.gpsimd.tensor_tensor(out=root[:], in0=sum_squares[:], in1=half_power[:], op=ALU.pow)
-            return root
+        def inverse(std_eps, inv_std, tiles):
+            cols = cols_of(tiles)
+            nc.vector.reciprocal(out=inv_std[:, cols], in_=std_eps[:, cols])
 
-        def root_of_squares(values, neg_mean):
-            sum_squares = small.tile([P, BT], F32, tag="sum_squares")
-            squares = work.tile([P, BT * UNITS], F32, tag="squares")
-            for t in range(BT):
-                sum_of_squares(values, neg_mean, squares, sum_squares, t)
-            return square_root(sum_squares)
-
-        def centre(values, neg_mean, gamma):
-            centred = work.tile([P, BT * UNITS], F32, tag="centred")
-            for t in range(BT):
+        def centre(values, neg_mean, gamma, centred, tiles):
+            for t in tiles:
                 nc.vector.scalar_tensor_tensor(
                     out=centred[:, block(t)],
                     in0=values[:, block(t)],
@@ -271,27 +301,9 @@ def tile_hyperlstmcell_pa_kernel(
                     op0=ALU.add,
                     op1=ALU.mult,
                 )
-            return centred
 
-        def std_plus_eps(root):
-            std_eps = small.tile([P, BT], F32, tag="std_eps")
-            nc.vector.tensor_scalar(
-                out=std_eps[:],
-                in0=root[:],
-                scalar1=1.0 / math.sqrt(UNITS - 1),
-                scalar2=EPS,
-                op0=ALU.mult,
-                op1=ALU.add,
-            )
-            return std_eps
-
-        def inverse(std_eps):
-            inv_std = small.tile([P, BT], F32, tag="inv_std")
-            nc.vector.reciprocal(out=inv_std[:], in_=std_eps[:])
-            return inv_std
-
-        def scale_and_shift(centred, inv_std, beta, out):
-            for t in range(BT):
+        def scale_and_shift(centred, inv_std, beta, out, tiles):
+            for t in tiles:
                 nc.vector.scalar_tensor_tensor(
                     out=out[:, block(t)],
                     in0=centred[:, block(t)],
@@ -301,167 +313,157 @@ def tile_hyperlstmcell_pa_kernel(
                     op1=ALU.add,
                 )
 
-        def gate_sums(gate):
-            v = work.tile([P, BT * UNITS], F32, tag="v")
-            v_sums = small.tile([P, BT], F32, tag="v_sums")
-            for pair in range(BT // 2):
-                bank = mx_psum.tile([P, BANK], F32, tag="mx")
-                for i in range(2):
-                    t = 2 * pair + i
-                    for g in range(PASSES):
-                        u_cols = slice(g * BATCH + t * P, g * BATCH + (t + 1) * P)
-                        w_cols = slice((gate * PASSES + g) * UNITS, (gate * PASSES + g + 1) * UNITS)
-                        nc.tensor.matmul_mx(
-                            out=bank[:, i * UNITS : (i + 1) * UNITS],
-                            lhsT=u_codes[:, u_cols].bitcast(FP8X4),
-                            lhsT_scale=u_scales[:, u_cols],
-                            rhs=w_codes[:, w_cols].bitcast(FP8X4),
-                            rhs_scale=w_scales[:, w_cols],
-                            start=(g == 0),
-                            stop=(g == PASSES - 1),
-                        )
-                for i in range(2):
-                    t = 2 * pair + i
-                    nc.vector.scalar_tensor_tensor(
-                        out=v[:, block(t)],
-                        in0=bank[:, i * UNITS : (i + 1) * UNITS],
-                        scalar=1.0,
-                        in1=plain[:, (gate * BT + t) * UNITS : (gate * BT + t + 1) * UNITS],
-                        op0=ALU.mult,
-                        op1=ALU.add,
-                        accum_out=v_sums[:, t : t + 1],
+        ALL = range(BT)
+        FIRST = range(0, BT // 2)
+        LAST = range(BT // 2, BT)
+
+        def column_tiles(what):
+            return [small.tile([P, BT], F32, name="%s%d" % (what, gate)) for gate in range(GATES + 1)]
+
+        CELL = GATES
+        sums = column_tiles("sums")
+        neg_means = column_tiles("neg_mean")
+        sum_squares = column_tiles("sum_squares")
+        roots = column_tiles("root")
+        std_epss = column_tiles("std_eps")
+        inv_stds = column_tiles("inv_std")
+        vs = [keep.tile([P, BT * UNITS], F32, name="v%d" % gate) for gate in range(GATES)]
+
+        def mx_product(gate, tiles):
+            bank = mx_psum.tile([P, BANK], F32, tag="mx")
+            for i, t in enumerate(tiles):
+                for g in range(PASSES):
+                    u_cols = slice(g * BATCH + t * P, g * BATCH + (t + 1) * P)
+                    w_cols = slice((gate * PASSES + g) * UNITS, (gate * PASSES + g + 1) * UNITS)
+                    nc.tensor.matmul_mx(
+                        out=bank[:, i * UNITS : (i + 1) * UNITS],
+                        lhsT=u_codes[:, u_cols].bitcast(FP8X4),
+                        lhsT_scale=u_scales[:, u_cols],
+                        rhs=w_codes[:, w_cols].bitcast(FP8X4),
+                        rhs_scale=w_scales[:, w_cols],
+                        start=(g == 0),
+                        stop=(g == PASSES - 1),
                     )
-            return v, v_sums
+            return bank
+
+        def add_up(gate, bank, t):
+            nc.vector.scalar_tensor_tensor(
+                out=vs[gate][:, block(t)],
+                in0=bank[:, (t % 2) * UNITS : (t % 2 + 1) * UNITS],
+                scalar=1.0,
+                in1=plain[:, t * N + gate * UNITS : t * N + (gate + 1) * UNITS],
+                op0=ALU.mult,
+                op1=ALU.add,
+                accum_out=sums[gate][:, t : t + 1],
+            )
 
         def gate_cols(gate):
             return slice(gate * UNITS, (gate + 1) * UNITS)
 
-        gates = [keep.tile([P, BT * UNITS], F32, name="gate%d" % gate) for gate in range(VECTOR_GATES)]
+        def squares_of(gate, tiles):
+            squares = work.tile([P, BT * UNITS], F32, tag="squares")
+            sum_of_squares(vs[gate], sums[gate], squares, sum_squares[gate], tiles)
 
-        def activate(gate, normed):
-            if gate == 1:
-                nc.scalar.activation(out=gates[gate][:], in_=normed[:], func=ACT.Sigmoid, bias=one_column[:])
-            else:
-                nc.scalar.activation(out=gates[gate][:], in_=normed[:], func=ACT.Sigmoid)
+        centred = work.tile([P, BT * UNITS], F32)
+        normed = work.tile([P, BT * UNITS], F32)
+        gate_g = keep.tile([P, BT * UNITS], F32)
 
-        def row_scale_and_bias(neg_mean, root):
-            inv_std = inverse(std_plus_eps(root))
-            neg_mean_over_std = small.tile([P, BT], F32, tag="neg_mean_over_std")
-            nc.vector.tensor_tensor(out=neg_mean_over_std[:], in0=neg_mean[:], in1=inv_std[:], op=ALU.mult)
-            return inv_std, neg_mean_over_std
+        def std_and_inverse(gate, tiles, filler=None):
+            std_plus_eps(roots[gate], std_epss[gate], tiles)
+            inverse(std_epss[gate], inv_stds[gate], tiles)
 
-        def gate_by_transposes(gate, func, v, inv_std, neg_mean_over_std, result_psum, result_tag):
-            normed = work.tile([P, BT * UNITS], F32, tag="normed")
-            flipped = []
-            for pair in range(BT // 2):
-                bank = flip_psum.tile([P, BANK], F32, tag="flip")
-                for i in range(2):
-                    t = 2 * pair + i
+        normeds = {}
+        gate_pool = stack.enter_context(tc.tile_pool(name="gate_pool", bufs=6))
+
+        def normalise(gate, tiles, on_gpsimd):
+            for t in tiles:
+                if on_gpsimd:
+                    nc.gpsimd.tensor_scalar(
+                        out=normeds[gate][:, block(t)],
+                        in0=vs[gate][:, block(t)],
+                        scalar1=neg_means[gate][:, t : t + 1],
+                        scalar2=inv_stds[gate][:, t : t + 1],
+                        op0=ALU.add,
+                        op1=ALU.mult,
+                    )
+                else:
                     nc.scalar.activation(
-                        out=normed[:, block(t)],
-                        in_=v[:, block(t)],
+                        out=normeds[gate][:, block(t)],
+                        in_=vs[gate][:, block(t)],
                         func=ACT.Identity,
-                        scale=inv_std[:, t : t + 1],
-                        bias=neg_mean_over_std[:, t : t + 1],
+                        scale=inv_stds[gate][:, t : t + 1],
+                        bias=neg_mean_over_stds[gate][:, t : t + 1],
                     )
-                for c in range(GATE_CHUNKS):
-                    for i in range(2):
-                        t = 2 * pair + i
-                        nc.tensor.transpose(
-                            out=bank[:, (2 * c + i) * P : (2 * c + i + 1) * P],
-                            in_=normed[:, t * UNITS + c * P : t * UNITS + (c + 1) * P],
-                            identity=ident_f32[:],
-                        )
-                flipped.append(bank)
-            gate_t = work.tile([P, BT * UNITS], F32, tag="gate_t")
-            result = []
-            for pair in range(BT // 2):
-                for c in range(GATE_CHUNKS):
-                    gamma_chunk = GAMMA_CHUNK + gate * GATE_CHUNKS + c
-                    beta_chunk = BETA_CHUNK + gate * GATE_CHUNKS + c
-                    nc.scalar.activation(
-                        out=gate_t[:, (2 * pair + c) * UNITS : (2 * pair + c + 1) * UNITS],
-                        in_=flipped[pair][:, c * UNITS : (c + 1) * UNITS],
-                        func=func,
-                        scale=norm_cols_f32[:, gamma_chunk : gamma_chunk + 1],
-                        bias=norm_cols_f32[:, beta_chunk : beta_chunk + 1],
+
+        neg_mean_over_stds = column_tiles("neg_mean_over_std")
+
+        def mean_over_std(gate, tiles):
+            cols = cols_of(tiles)
+            nc.vector.tensor_tensor(
+                out=neg_mean_over_stds[gate][:, cols],
+                in0=neg_means[gate][:, cols],
+                in1=inv_stds[gate][:, cols],
+                op=ALU.mult,
+            )
+
+        def turn(gate, tiles):
+            bank = flip_psum.tile([P, BANK], F32, tag="flip")
+            for c in range(GATE_CHUNKS):
+                for i, t in enumerate(tiles):
+                    nc.tensor.transpose(
+                        out=bank[:, (2 * c + i) * P : (2 * c + i + 1) * P],
+                        in_=normeds[gate][:, t * UNITS + c * P : t * UNITS + (c + 1) * P],
+                        identity=ident_f32[:],
                     )
-                bank = result_psum.tile([P, BANK], F32, tag=result_tag)
-                for i in range(2):
-                    for c in range(GATE_CHUNKS):
-                        first = (2 * pair + c) * UNITS + i * P
-                        nc.tensor.transpose(
-                            out=bank[:, i * UNITS + c * P : i * UNITS + (c + 1) * P],
-                            in_=gate_t[:, first : first + P],
-                            identity=ident_f32[:],
-                        )
-                result.append(bank)
+            return bank
+
+        def activate(gate, func, bank):
+            gate_t = gate_pool.tile([P, BANK], F32, tag="gate_t")
+            for c in range(GATE_CHUNKS):
+                gamma_chunk = GAMMA_CHUNK + gate * GATE_CHUNKS + c
+                beta_chunk = BETA_CHUNK + gate * GATE_CHUNKS + c
+                beta = (beta_plus_one if gate == 1 else norm_cols_f32)[:, beta_chunk : beta_chunk + 1]
+                nc.scalar.activation(
+                    out=gate_t[:, c * UNITS : (c + 1) * UNITS],
+                    in_=bank[:, c * UNITS : (c + 1) * UNITS],
+                    func=func,
+                    scale=norm_cols_f32[:, gamma_chunk : gamma_chunk + 1],
+                    bias=beta,
+                )
+            return gate_t
+
+        def turn_back(gate_t, back_psum=mx_psum, back_tag="mx"):
+            result = back_psum.tile([P, BANK], F32, tag=back_tag)
+            for i in range(2):
+                for c in range(GATE_CHUNKS):
+                    first = c * UNITS + i * P
+                    nc.tensor.transpose(
+                        out=result[:, i * UNITS + c * P : i * UNITS + (c + 1) * P],
+                        in_=gate_t[:, first : first + P],
+                        identity=ident_f32[:],
+                    )
             return result
 
-        grouped_u = [flip_u(0), flip_u(1)]
-        quantise_u(0, grouped_u[0])
-        plain_product(0)
-        quantise_u(1, grouped_u[1])
-        grouped_u = grouped_u + [flip_u(2), flip_u(3)]
-        quantise_u(2, grouped_u[2])
-        quantise_u(3, grouped_u[3])
-        grouped_w = {0: flip_w(0, vector_helps=True)}
-        quantise_w(0, 0, grouped_w[0][0])
-        quantise_w(0, 1, grouped_w[0][1])
-        grouped_w[1] = flip_w(1, vector_helps=False)
-
-        vs = []
-        neg_means = []
-        roots = []
-        centreds = []
-        for gate in range(GATES - 1):
-            before = gate - 1
-            v, v_sums = gate_sums(gate)
-            vs.append(v)
-            neg_means.append(negated_mean(v_sums))
-            roots.append(root_of_squares(v, neg_means[gate]))
-            plain_product(gate + 1)
-            quantise_w(gate + 1, 0, grouped_w[gate + 1][0])
-            if before >= 0:
-                std_eps = std_plus_eps(roots[before])
-            quantise_w(gate + 1, 1, grouped_w[gate + 1][1])
-            if before >= 0:
-                inv_std = inverse(std_eps)
-            if gate < VECTOR_GATES:
-                centreds.append(centre(v, neg_means[gate], ln_gamma[:, gate_cols(gate)]))
-            if before >= 0:
-                normed = work.tile([P, BT * UNITS], F32, tag="normed")
-                scale_and_shift(centreds[before], inv_std, ln_beta[:, gate_cols(before)], normed)
-            if gate + 2 < GATES:
-                grouped_w[gate + 2] = flip_w(gate + 2, vector_helps=False)
-            if before >= 0:
-                activate(before, normed)
-
-        late = flip_psum.tile([P, 2 * BANK], BF16, tag="flip")
-        spread_chunks(late[:, 0:UNITS], LNC_GAMMA_CHUNK, GATE_CHUNKS)
-        spread_chunks(late[:, UNITS : 2 * UNITS], LNC_BETA_CHUNK, GATE_CHUNKS)
-        lnc_gamma = late[:, 0:UNITS]
-        lnc_beta = late[:, UNITS : 2 * UNITS]
-
-        inv_std, neg_mean_over_std = row_scale_and_bias(neg_means[2], roots[2])
-        v, v_sums = gate_sums(3)
-        gate_g = gate_by_transposes(2, ACT.Tanh, vs[2], inv_std, neg_mean_over_std, mx_psum, "mx")
-        neg_mean = negated_mean(v_sums)
         kept = keep.tile([P, BT * UNITS], F32)
-        nc.vector.tensor_tensor(out=kept[:], in0=gates[1][:], in1=c_raw[:], op=ALU.mult)
-        root = root_of_squares(v, neg_mean)
-
         fresh = keep.tile([P, BT * UNITS], F32)
-        for pair in range(BT // 2):
-            cols = slice(pair * BANK, (pair + 1) * BANK)
-            nc.vector.tensor_tensor(out=fresh[:, cols], in0=gates[0][:, cols], in1=gate_g[pair][:], op=ALU.mult)
         cell = keep.tile([P, BT * UNITS], F32)
-        cell_sums = small.tile([P, BT], F32)
-        cell_neg_mean = small.tile([P, BT], F32)
-        cell_sum_squares = small.tile([P, BT], F32)
-        squares = work.tile([P, BT * UNITS], F32, tag="squares")
-        for t in range(BT + 1):
-            if t < BT:
+        cell_centred = keep.tile([P, BT * UNITS], F32)
+        new_c = keep.tile([P, BT * UNITS], F32)
+        tanh_c = keep.tile([P, BT * UNITS], F32)
+        new_h = keep.tile([P, BT * UNITS], F32)
+        cell_squares = keep.tile([P, BT * UNITS], F32)
+        out_0_tiles = out_0.rearrange("(p t) n -> p t n", t=BT)
+        out_1_tiles = out_1.rearrange("(p t) n -> p t n", t=BT)
+
+        def pair_cols(tiles):
+            return slice(tiles.start * UNITS, tiles.stop * UNITS)
+
+        def product(out, values, psum, tiles):
+            cols = pair_cols(tiles)
+            nc.vector.tensor_tensor(out=out[:, cols], in0=values[:, cols], in1=psum[:], op=ALU.mult)
+
+        def cell_sum(tiles):
+            for t in tiles:
                 nc.vector.scalar_tensor_tensor(
                     out=cell[:, block(t)],
                     in0=kept[:, block(t)],
@@ -469,27 +471,151 @@ def tile_hyperlstmcell_pa_kernel(
                     in1=fresh[:, block(t)],
                     op0=ALU.mult,
                     op1=ALU.add,
-                    accum_out=cell_sums[:, t : t + 1],
+                    accum_out=sums[CELL][:, t : t + 1],
                 )
-            if t >= 1:
-                done = slice(t - 1, t)
-                nc.vector.tensor_scalar_mul(out=cell_neg_mean[:, done], in0=cell_sums[:, done], scalar1=-1.0 / UNITS)
-                sum_of_squares(cell, cell_neg_mean, squares, cell_sum_squares, t - 1)
-        cell_root = square_root(cell_sum_squares)
 
-        inv_std, neg_mean_over_std = row_scale_and_bias(neg_mean, root)
-        gate_o = gate_by_transposes(3, ACT.Sigmoid, v, inv_std, neg_mean_over_std, plain_psum, "plain")
+        s_copy = nc.scalar.copy
+        v_copy = nc.vector.tensor_copy
+        W = {}
+        U = [new_grouped() for g in range(PASSES)]
+        flip_u(0, 0, U[0], s_copy)
+        flip_u(1, 0, U[1], s_copy)
+        flip_u(0, 1, U[0], s_copy)
+        flip_u(1, 1, U[1], s_copy)
+        turn_hyper_h()
+        turn_norm_rows()
+        turn_whh(0)
+        turn_whh(1)
+        spread_bias()
+        quantise_u(0, U[0])
+        quantise_u(1, U[1])
+        plain_product(0, 0)
+        flip_u(2, 0, U[2], s_copy)
+        flip_u(3, 0, U[3], s_copy)
+        plain_product(0, 1)
+        flip_u(2, 1, U[2], s_copy)
+        flip_u(3, 1, U[3], s_copy)
+        plain_product(0, 2)
+        for gate, i in ((0, 0), (0, 1), (1, 0)):
+            W[gate, i] = new_grouped()
+            for b in range(2):
+                flip_w(gate, i, b, W[gate, i], s_copy)
+            if (gate, i) == (0, 0):
+                quantise_u(2, U[2])
+                plain_product(0, 3)
+                quantise_u(3, U[3])
+            if (gate, i) == (0, 1):
+                quantise_w(0, 0, W[0, 0])
+                plain_product(1, 0)
+        quantise_w(0, 1, W[0, 1])
 
-        cell_centred = centre(cell, cell_neg_mean, lnc_gamma)
-        new_c = keep.tile([P, BT * UNITS], F32)
-        scale_and_shift(cell_centred, inverse(std_plus_eps(cell_root)), lnc_beta, new_c)
-        out_0_tiles = out_0.rearrange("(p t) n -> p t n", t=BT)
-        out_1_tiles = out_1.rearrange("(p t) n -> p t n", t=BT)
-        for t in range(BT):
-            nc.sync.dma_start(out=out_1_tiles[:, t, :], in_=new_c[:, block(t)])
-        tanh_c = keep.tile([P, BT * UNITS], F32)
-        new_h = keep.tile([P, BT * UNITS], F32)
-        for t in range(BT):
+        FUNC = (ACT.Sigmoid, ACT.Sigmoid, ACT.Tanh, ACT.Sigmoid)
+        units = [(gate, tiles) for gate in range(GATES) for tiles in (FIRST, LAST)]
+        turned = {}
+        gate_t = {}
+        backs = {}
+        for gate in range(GATES):
+            normeds[gate] = keep.tile([P, BT * UNITS], F32, name="normed%d" % gate)
+
+        def std_of(s):
+            gate, tiles = units[s]
+            std_plus_eps(roots[gate], std_epss[gate], tiles)
+
+        def inverse_of(s):
+            gate, tiles = units[s]
+            inverse(std_epss[gate], inv_stds[gate], tiles)
+
+        def fresh_half(k):
+            cols = pair_cols((FIRST, LAST)[k])
+            nc.vector.tensor_tensor(out=fresh[:, cols], in0=gate_t[k][:], in1=gate_t[4 + k][:], op=ALU.mult)
+            backs[4 + k] = turn_back(fresh[:, cols], plain_psum, "plain")
+
+        def kept_half(k):
+            product(kept, c_raw, backs[2 + k], (FIRST, LAST)[k])
+
+        for s, (gate, tiles) in enumerate(units):
+            half = s % 2
+            bank = mx_product(gate, tiles)
+            ahead = (gate + 1, 1) if half == 0 else (gate + 2, 0)
+            if ahead[0] < GATES:
+                W[ahead] = new_grouped()
+                flip_w(ahead[0], ahead[1], 0, W[ahead], s_copy)
+            add_up(gate, bank, tiles[0])
+            if s >= 1:
+                std_of(s - 1)
+            add_up(gate, bank, tiles[1])
+            if s >= 1:
+                inverse_of(s - 1)
+                normalise(units[s - 1][0], units[s - 1][1], True)
+            squares_of(gate, tiles)
+            square_root(sum_squares[gate], roots[gate], tiles)
+            if ahead[0] < GATES:
+                flip_w(ahead[0], ahead[1], 1, W[ahead], s_copy)
+            if gate + 1 < GATES:
+                quantise_w(gate + 1, half, W[gate + 1, half])
+            if s < 3:
+                plain_product(1, 1 + s)
+            negated_mean(sums[gate], neg_means[gate], tiles)
+            if s >= 2:
+                turned[s - 2] = turn(units[s - 2][0], units[s - 2][1])
+                gate_t[s - 2] = activate(units[s - 2][0], FUNC[units[s - 2][0]], turned[s - 2])
+            if 4 <= s - 1 < 6:
+                backs[s - 3] = turn_back(gate_t[s - 3], plain_psum, "plain")
+            if s == 6:
+                kept_half(0)
+            if s == 7:
+                fresh_half(0)
+                kept_half(1)
+
+        late = flip_psum.tile([P, 2 * BANK], BF16, tag="flip")
+        spread_chunks(late[:, 0:UNITS], LNC_GAMMA_CHUNK, GATE_CHUNKS)
+        spread_chunks(late[:, UNITS : 2 * UNITS], LNC_BETA_CHUNK, GATE_CHUNKS)
+        lnc_gamma = late[:, 0:UNITS]
+        lnc_beta = late[:, UNITS : 2 * UNITS]
+
+        def cell_sum(t):
+            nc.vector.scalar_tensor_tensor(
+                out=cell[:, block(t)],
+                in0=backs[4 + t // 2][:, (t % 2) * UNITS : (t % 2 + 1) * UNITS],
+                scalar=1.0,
+                in1=kept[:, block(t)],
+                op0=ALU.mult,
+                op1=ALU.add,
+                accum_out=sums[CELL][:, t : t + 1],
+            )
+
+        def cell_square(tiles):
+            sum_of_squares(cell, sums[CELL], cell_squares, sum_squares[CELL], tiles)
+            square_root(sum_squares[CELL], roots[CELL], tiles)
+
+        std_of(7)
+        fresh_half(1)
+        cell_sum(0)
+        inverse_of(7)
+        cell_sum(1)
+        cell_square(FIRST)
+        normalise(units[7][0], units[7][1], True)
+        negated_mean(sums[CELL], neg_means[CELL], FIRST)
+        turned[6] = turn(3, FIRST)
+        gate_t[6] = activate(3, FUNC[3], turned[6])
+        cell_sum(2)
+        cell_sum(3)
+        cell_square(LAST)
+        centre(cell, neg_means[CELL], lnc_gamma, cell_centred, FIRST)
+        negated_mean(sums[CELL], neg_means[CELL], LAST)
+        turned[7] = turn(3, LAST)
+        gate_t[7] = activate(3, FUNC[3], turned[7])
+        std_plus_eps(roots[CELL], std_epss[CELL], FIRST)
+        centre(cell, neg_means[CELL], lnc_gamma, cell_centred, range(2, 3))
+        inverse(std_epss[CELL], inv_stds[CELL], FIRST)
+        centre(cell, neg_means[CELL], lnc_gamma, cell_centred, range(3, 4))
+        scale_and_shift(cell_centred, inv_stds[CELL], lnc_beta, new_c, range(0, 1))
+        std_plus_eps(roots[CELL], std_epss[CELL], LAST)
+        scale_and_shift(cell_centred, inv_stds[CELL], lnc_beta, new_c, range(1, 2))
+        inverse(std_epss[CELL], inv_stds[CELL], LAST)
+        gate_o = [turn_back(gate_t[6]), turn_back(gate_t[7])]
+
+        def finish(t):
             nc.scalar.activation(out=tanh_c[:, block(t)], in_=new_c[:, block(t)], func=ACT.Tanh)
             nc.vector.tensor_tensor(
                 out=new_h[:, block(t)],
@@ -497,4 +623,12 @@ def tile_hyperlstmcell_pa_kernel(
                 in1=gate_o[t // 2][:, (t % 2) * UNITS : (t % 2 + 1) * UNITS],
                 op=ALU.mult,
             )
+
+        for t in FIRST:
+            nc.sync.dma_start(out=out_1_tiles[:, t, :], in_=new_c[:, block(t)])
+        scale_and_shift(cell_centred, inv_stds[CELL], lnc_beta, new_c, LAST)
+        for t in LAST:
+            nc.sync.dma_start(out=out_1_tiles[:, t, :], in_=new_c[:, block(t)])
+        for t in ALL:
+            finish(t)
             nc.sync.dma_start(out=out_0_tiles[:, t, :], in_=new_h[:, block(t)])

@@ -65,6 +65,10 @@ def tile_hyperlstmcell_pa_kernel(
 
         norm_rows = consts.tile([P, P], BF16)
         nc.vector.memset(norm_rows[:], 0.0)
+        ones = consts.tile([P, P], BF16)
+        nc.vector.memset(ones[:], 1.0)
+        bias_row = consts.tile([P, UNITS], BF16)
+        nc.vector.memset(bias_row[:], 0.0)
         half_power = consts.tile([P, BT], F32)
         nc.vector.memset(half_power[:], 0.5)
         one_column = consts.tile([P, 1], F32)
@@ -76,6 +80,9 @@ def tile_hyperlstmcell_pa_kernel(
         table_warmer = consts.tile([P, 1], F32)
         nc.scalar.activation(out=table_warmer[:], in_=one_column[:], func=ACT.Sigmoid)
 
+        INPUT, FORGET, CELL_GATE, OUTPUT = range(GATES)
+        ORDER = (INPUT, CELL_GATE, FORGET, OUTPUT)
+
         GATE_CHUNKS = UNITS // P
         BIAS_CHUNK = 0
         GAMMA_CHUNK = BIAS_CHUNK + N // P
@@ -83,14 +90,18 @@ def tile_hyperlstmcell_pa_kernel(
         LNC_GAMMA_CHUNK = BETA_CHUNK + N // P
         LNC_BETA_CHUNK = LNC_GAMMA_CHUNK + GATE_CHUNKS
 
+        hh_raw = raw.tile([P, BT * UNITS], BF16)
+        nc.sync.dma_start(out=hh_raw[:], in_=hyper_h.rearrange("(p t) k -> p (t k)", t=BT))
         x_raw = raw.tile([P, BT * IN], BF16)
         h_raw = raw.tile([P, BT * IN], BF16)
         half_cols = (slice(0, BT // 2 * IN), slice(BT // 2 * IN, BT * IN))
         x_rows = x.rearrange("(p t) k -> p (t k)", t=BT)
-        for cols in half_cols:
-            nc.sync.dma_start(out=x_raw[:, cols], in_=x_rows[:, cols])
-        hh_raw = raw.tile([P, BT * UNITS], BF16)
-        nc.sync.dma_start(out=hh_raw[:], in_=hyper_h.rearrange("(p t) k -> p (t k)", t=BT))
+        nc.sync.dma_start(out=x_raw[:, half_cols[0]], in_=x_rows[:, half_cols[0]])
+        whh_raw = raw.tile([P, (N // P) * UNITS], BF16)
+        nc.sync.dma_start(
+            out=whh_raw[:].rearrange("p (j k) -> p j k", k=UNITS),
+            in_=hc_Whh.rearrange("(j p) k -> p j k", p=P),
+        )
         nc.sync.dma_start(out=norm_rows[BIAS_CHUNK:GAMMA_CHUNK, :], in_=hc_bih.rearrange("(c q) -> c q", q=P))
         nc.sync.dma_start(out=norm_rows[GAMMA_CHUNK:BETA_CHUNK, :], in_=hc_ln_gamma.rearrange("g (c q) -> (g c) q", q=P))
         nc.sync.dma_start(
@@ -103,22 +114,21 @@ def tile_hyperlstmcell_pa_kernel(
             out=norm_rows[LNC_BETA_CHUNK : LNC_BETA_CHUNK + GATE_CHUNKS, :],
             in_=hc_lnc_beta.rearrange("(c q) -> c q", q=P),
         )
-        whh_raw = raw.tile([P, (N // P) * UNITS], BF16)
         nc.sync.dma_start(
-            out=whh_raw[:].rearrange("p (j k) -> p j k", k=UNITS),
-            in_=hc_Whh.rearrange("(j p) k -> p j k", p=P),
+            out=bias_row[0:1, :], in_=hc_bih[OUTPUT * UNITS : (OUTPUT + 1) * UNITS].rearrange("(o n) -> o n", o=1)
         )
+        nc.sync.dma_start(out=x_raw[:, half_cols[1]], in_=x_rows[:, half_cols[1]])
         nc.sync.dma_start(out=h_raw[:], in_=h.rearrange("(p t) k -> p (t k)", t=BT))
         c_raw = raw.tile([P, BT * UNITS], BF16)
         w_raw = []
-        for gate in range(GATES):
-            w_gate = raw.tile([P, 2 * K], BF16, name="w_raw%d" % gate)
+        for position, gate in enumerate(ORDER):
+            w_gate = raw.tile([P, 2 * K], BF16, name="w_raw%d" % position)
             nc.sync.dma_start(
                 out=w_gate[:].rearrange("p (j k) -> p j k", k=K),
                 in_=hc_Wih[gate * UNITS : (gate + 1) * UNITS, :].rearrange("(j p) k -> p j k", p=P),
             )
             w_raw.append(w_gate)
-            if gate == 1:
+            if position == 1:
                 nc.sync.dma_start(out=c_raw[:], in_=hyper_c.rearrange("(p t) n -> p (t n)", t=BT))
 
         hh_t = operands.tile([P, KH * BT * P], BF16)
@@ -137,9 +147,10 @@ def tile_hyperlstmcell_pa_kernel(
 
         def turn_whh(step):
             bank = flip_psum.tile([P, 2 * BANK], BF16, tag="flip")
-            for j in range(N // P):
+            for slot in range(N // P):
+                j = ORDER[slot // GATE_CHUNKS] * GATE_CHUNKS + slot % GATE_CHUNKS
                 nc.tensor.transpose(
-                    out=bank[:, j * P : (j + 1) * P],
+                    out=bank[:, slot * P : (slot + 1) * P],
                     in_=whh_raw[:, j * UNITS + step * P : j * UNITS + (step + 1) * P],
                     identity=ident_bf16[:],
                 )
@@ -147,59 +158,94 @@ def tile_hyperlstmcell_pa_kernel(
 
         norm_cols = consts.tile([P, P], BF16)
         norm_cols_f32 = consts.tile([P, P], F32)
-        beta_plus_one = consts.tile([P, P], F32)
 
         def turn_norm_rows():
             bank = flip_psum.tile([P, 2 * BANK], BF16, tag="flip")
             nc.tensor.transpose(out=bank[:, 0:P], in_=norm_rows[:], identity=ident_bf16[:])
             nc.vector.tensor_copy(out=norm_cols[:], in_=bank[:, 0:P])
             nc.vector.tensor_copy(out=norm_cols_f32[:], in_=bank[:, 0:P])
-            nc.vector.tensor_scalar(
-                out=beta_plus_one[:], in0=bank[:, 0:P], scalar1=1.0, scalar2=1.0, op0=ALU.mult, op1=ALU.add
-            )
 
-        def spread_chunks(bank, first, chunks):
-            for i in range(chunks):
+        def spread_chunks(bank, chunks):
+            for i, chunk in enumerate(chunks):
                 nc.tensor.transpose(
                     out=bank[:, i * P : (i + 1) * P],
-                    in_=norm_cols[:, first + i : first + i + 1].to_broadcast([P, P]),
+                    in_=norm_cols[:, chunk : chunk + 1].to_broadcast([P, P]),
                     identity=ident_bf16[:],
                 )
+
+        def gate_chunks(first, gate):
+            return [first + gate * GATE_CHUNKS + c for c in range(GATE_CHUNKS)]
 
         bias = consts.tile([P, N], BF16)
 
         def spread_bias():
             bank = flip_psum.tile([P, 2 * BANK], BF16, tag="flip")
-            spread_chunks(bank[:], BIAS_CHUNK, N // P)
+            spread_chunks(bank[:], [chunk for gate in ORDER for chunk in gate_chunks(BIAS_CHUNK, gate)])
             nc.vector.tensor_copy(out=bias[:], in_=bank[:])
 
-        CELL_GATE = 2
-        ln_vectors = consts.tile([P, 2 * UNITS], BF16)
-        ln_gamma = ln_vectors[:, 0:UNITS]
-        ln_beta = ln_vectors[:, UNITS : 2 * UNITS]
+        VECTOR_GATES = (FORGET,)
+        ln_vectors = consts.tile([P, BANK], BF16)
 
         def spread_norm_vectors():
             bank = flip_psum.tile([P, 2 * BANK], BF16, tag="flip")
-            spread_chunks(bank[:, 0:UNITS], GAMMA_CHUNK + CELL_GATE * GATE_CHUNKS, GATE_CHUNKS)
-            spread_chunks(bank[:, UNITS : 2 * UNITS], BETA_CHUNK + CELL_GATE * GATE_CHUNKS, GATE_CHUNKS)
-            nc.vector.tensor_copy(out=ln_vectors[:], in_=bank[:, 0 : 2 * UNITS])
+            spread_chunks(
+                bank[:],
+                [chunk for first in (GAMMA_CHUNK, BETA_CHUNK) for gate in VECTOR_GATES for chunk in gate_chunks(first, gate)],
+            )
+            nc.vector.tensor_copy(out=ln_vectors[:], in_=bank[:, 0:BANK])
+
+        def gate_vector(which, position):
+            first = (which * len(VECTOR_GATES) + VECTOR_GATES.index(ORDER[position])) * UNITS
+            return ln_vectors[:, first : first + UNITS]
 
         plain = operands.tile([P, BT * N], F32)
 
-        def plain_product(gate_pair, t):
-            units = slice(gate_pair * BANK, (gate_pair + 1) * BANK)
-            bank = plain_psum.tile([P, BANK], F32, tag="plain")
+        def plain_columns(position, t):
+            first = t * N + position * UNITS
+            return plain[:, first : first + UNITS]
+
+        def plain_matmuls(group, t, units, closed):
             for step in range(KH):
                 nc.tensor.matmul(
-                    out=bank[:],
+                    out=group,
                     lhsT=hh_t[:, (step * BT + t) * P : (step * BT + t + 1) * P],
                     rhs=whh_t[:, step * N + units.start : step * N + units.stop],
                     start=(step == 0),
-                    stop=(step == KH - 1),
+                    stop=(step == KH - 1 and closed),
                 )
+
+        def plain_first_two(t):
+            units = slice(0, BANK)
+            bank = plain_psum.tile([P, BANK], F32, tag="plain")
+            plain_matmuls(bank[:], t, units, True)
             nc.vector.tensor_tensor(
-                out=plain[:, t * N + units.start : t * N + units.stop], in0=bank[:], in1=bias[:, units], op=ALU.add
+                out=plain[:, t * N : t * N + BANK], in0=bank[:], in1=bias[:, units], op=ALU.add
             )
+
+        def plain_third(tiles):
+            units = slice(2 * UNITS, 3 * UNITS)
+            bank = plain_psum.tile([P, BANK], F32, tag="plain")
+            for i, t in enumerate(tiles):
+                plain_matmuls(bank[:, i * UNITS : (i + 1) * UNITS], t, units, True)
+            for i, t in enumerate(tiles):
+                nc.vector.tensor_tensor(
+                    out=plain_columns(2, t), in0=bank[:, i * UNITS : (i + 1) * UNITS], in1=bias[:, units], op=ALU.add
+                )
+
+        last_banks = {}
+
+        def plain_last_matmuls(tiles):
+            units = slice(3 * UNITS, 4 * UNITS)
+            bank = plain_psum.tile([P, BANK], F32, tag="plain")
+            for i, t in enumerate(tiles):
+                group = bank[:, i * UNITS : (i + 1) * UNITS]
+                plain_matmuls(group, t, units, False)
+                nc.tensor.matmul(out=group, lhsT=ones[:], rhs=bias_row[:], start=False, stop=True)
+            last_banks[tiles.start] = bank
+
+        def plain_last_copies(tiles):
+            for i, t in enumerate(tiles):
+                nc.scalar.copy(out=plain_columns(3, t), in_=last_banks[tiles.start][:, i * UNITS : (i + 1) * UNITS])
 
         u_codes = operands.tile([P, PASSES * BATCH], U32, align_bytes=64)
         u_scales = operands.tile([P, PASSES * BATCH], U8, align_bytes=64)
@@ -228,21 +274,21 @@ def tile_hyperlstmcell_pa_kernel(
             grouped = stage.tile([P, 2 * BANK * 2], BF16, align_bytes=64, tag="grouped")
             return grouped
 
-        def flip_u(g, b, grouped, copy):
-            words = (x_raw if g < PASSES // 2 else h_raw)[:].bitcast(F32)
-            firsts = [t * X_WORDS + (g % (PASSES // 2)) * PASS_WORDS for t in (2 * b, 2 * b + 1)]
-            flip_piece(grouped, b, [every_second(words, first) for first in firsts], copy)
-
         def every_second(words, first):
             return lambda parity: words[:, first + parity : first + PASS_WORDS : 2]
 
-        def w_half(gate, j, g):
-            words = w_raw[gate][:].bitcast(F32)
-            first = j * ROW_WORDS + g * PASS_WORDS
-            return lambda parity: words[:, first + parity : first + PASS_WORDS : 2]
+        def flip_u(g, b, grouped, copy):
+            which, g_in = divmod(g, PASSES // 2)
+            pair = (2 * b, 2 * b + 1)
+            words = (x_raw, h_raw)[which][:].bitcast(F32)
+            views = [every_second(words, t * X_WORDS + g_in * PASS_WORDS) for t in pair]
+            flip_piece(grouped, b, views, copy)
 
-        def flip_w(gate, i, b, grouped, copy):
-            flip_piece(grouped, b, [w_half(gate, j, 2 * i + b) for j in range(2)], copy)
+        def flip_w(position, i, b, grouped, copy):
+            g = 2 * i + b
+            words = w_raw[position][:].bitcast(F32)
+            views = [every_second(words, j * ROW_WORDS + g * PASS_WORDS) for j in range(2)]
+            flip_piece(grouped, b, views, copy)
 
         def quantise_u(g, grouped):
             cols = slice(g * BATCH, (g + 1) * BATCH)
@@ -364,9 +410,6 @@ def tile_hyperlstmcell_pa_kernel(
             squares = work.tile([P, BT * UNITS], F32, tag="squares")
             sum_of_squares(vs[gate], sums[gate], squares, sum_squares[gate], tiles)
 
-        centred = work.tile([P, BT * UNITS], F32)
-        normed = work.tile([P, BT * UNITS], F32)
-        gate_g = keep.tile([P, BT * UNITS], F32)
 
         def std_and_inverse(gate, tiles, filler=None):
             std_plus_eps(roots[gate], std_epss[gate], tiles)
@@ -420,9 +463,9 @@ def tile_hyperlstmcell_pa_kernel(
         def activate(gate, func, bank):
             gate_t = gate_pool.tile([P, BANK], F32, tag="gate_t")
             for c in range(GATE_CHUNKS):
-                gamma_chunk = GAMMA_CHUNK + gate * GATE_CHUNKS + c
-                beta_chunk = BETA_CHUNK + gate * GATE_CHUNKS + c
-                beta = (beta_plus_one if gate == 1 else norm_cols_f32)[:, beta_chunk : beta_chunk + 1]
+                gamma_chunk = GAMMA_CHUNK + ORDER[gate] * GATE_CHUNKS + c
+                beta_chunk = BETA_CHUNK + ORDER[gate] * GATE_CHUNKS + c
+                beta = norm_cols_f32[:, beta_chunk : beta_chunk + 1]
                 nc.scalar.activation(
                     out=gate_t[:, c * UNITS : (c + 1) * UNITS],
                     in_=bank[:, c * UNITS : (c + 1) * UNITS],
@@ -451,7 +494,6 @@ def tile_hyperlstmcell_pa_kernel(
         new_c = keep.tile([P, BT * UNITS], F32)
         tanh_c = keep.tile([P, BT * UNITS], F32)
         new_h = keep.tile([P, BT * UNITS], F32)
-        cell_squares = keep.tile([P, BT * UNITS], F32)
         out_0_tiles = out_0.rearrange("(p t) n -> p t n", t=BT)
         out_1_tiles = out_1.rearrange("(p t) n -> p t n", t=BT)
 
@@ -475,108 +517,101 @@ def tile_hyperlstmcell_pa_kernel(
                 )
 
         s_copy = nc.scalar.copy
-        v_copy = nc.vector.tensor_copy
         W = {}
         U = [new_grouped() for g in range(PASSES)]
+
+        def flip_w_half(position, i, b):
+            if b == 0:
+                W[position, i] = new_grouped()
+            flip_w(position, i, b, W[position, i], s_copy)
+
+        turn_hyper_h()
         flip_u(0, 0, U[0], s_copy)
         flip_u(1, 0, U[1], s_copy)
-        flip_u(0, 1, U[0], s_copy)
-        flip_u(1, 1, U[1], s_copy)
-        turn_hyper_h()
-        turn_norm_rows()
         turn_whh(0)
         turn_whh(1)
-        spread_bias()
+        turn_norm_rows()
+        flip_u(0, 1, U[0], s_copy)
+        flip_u(1, 1, U[1], s_copy)
         quantise_u(0, U[0])
         quantise_u(1, U[1])
-        plain_product(0, 0)
-        flip_u(2, 0, U[2], s_copy)
-        flip_u(3, 0, U[3], s_copy)
-        plain_product(0, 1)
-        flip_u(2, 1, U[2], s_copy)
-        flip_u(3, 1, U[3], s_copy)
-        plain_product(0, 2)
-        for gate, i in ((0, 0), (0, 1), (1, 0)):
-            W[gate, i] = new_grouped()
-            for b in range(2):
-                flip_w(gate, i, b, W[gate, i], s_copy)
-            if (gate, i) == (0, 0):
-                quantise_u(2, U[2])
-                plain_product(0, 3)
-                quantise_u(3, U[3])
-            if (gate, i) == (0, 1):
-                quantise_w(0, 0, W[0, 0])
-                plain_product(1, 0)
+        spread_bias()
+        plain_first_two(0)
+        for b in range(2):
+            flip_u(2, b, U[2], s_copy)
+            flip_u(3, b, U[3], s_copy)
+        flip_w_half(0, 0, 0)
+        flip_w_half(0, 0, 1)
+        plain_first_two(1)
+        quantise_u(2, U[2])
+        quantise_u(3, U[3])
+        flip_w_half(0, 1, 0)
+        flip_w_half(0, 1, 1)
+        quantise_w(0, 0, W[0, 0])
+        plain_first_two(2)
+        spread_norm_vectors()
+        flip_w_half(1, 0, 0)
+        flip_w_half(1, 0, 1)
         quantise_w(0, 1, W[0, 1])
 
-        FUNC = (ACT.Sigmoid, ACT.Sigmoid, ACT.Tanh, ACT.Sigmoid)
-        units = [(gate, tiles) for gate in range(GATES) for tiles in (FIRST, LAST)]
-        turned = {}
+        FUNC = (ACT.Sigmoid, ACT.Tanh, ACT.Sigmoid, ACT.Sigmoid)
+        units = [(position, tiles) for position in range(GATES) for tiles in (FIRST, LAST)]
+        for position in (0, 1, 3):
+            normeds[position] = keep.tile([P, BT * UNITS], F32, name="normed%d" % position)
+        centred = keep.tile([P, BT * UNITS], F32)
+        gate_f = keep.tile([P, BT * UNITS], F32)
         gate_t = {}
         backs = {}
-        for gate in range(GATES):
-            normeds[gate] = keep.tile([P, BT * UNITS], F32, name="normed%d" % gate)
 
         def std_of(s):
-            gate, tiles = units[s]
-            std_plus_eps(roots[gate], std_epss[gate], tiles)
+            position, tiles = units[s]
+            std_plus_eps(roots[position], std_epss[position], tiles)
 
         def inverse_of(s):
-            gate, tiles = units[s]
-            inverse(std_epss[gate], inv_stds[gate], tiles)
+            position, tiles = units[s]
+            inverse(std_epss[position], inv_stds[position], tiles)
+
+        def squares_and_root(s):
+            position, tiles = units[s]
+            squares_of(position, tiles)
+            square_root(sum_squares[position], roots[position], tiles)
+
+        def mean_of(s):
+            position, tiles = units[s]
+            negated_mean(sums[position], neg_means[position], tiles)
+
+        def normalise_of(s, on_gpsimd=True):
+            normalise(units[s][0], units[s][1], on_gpsimd)
+
+        def turn_and_activate(s):
+            position, tiles = units[s]
+            gate_t[s] = activate(position, FUNC[position], turn(position, tiles))
+
+        def forget_centre(tiles):
+            centre(vs[2], neg_means[2], gate_vector(0, 2), centred, tiles)
+
+        def forget_finish(tiles):
+            cols = pair_cols(tiles)
+            normed = work.tile([P, BT * UNITS], F32, tag="normed")
+            scale_and_shift(centred, inv_stds[2], gate_vector(1, 2), normed, tiles)
+            nc.scalar.activation(out=gate_f[:, cols], in_=normed[:, cols], func=ACT.Sigmoid, bias=one_column[:])
+
+        def kept_half(tiles):
+            cols = pair_cols(tiles)
+            nc.vector.tensor_tensor(out=kept[:, cols], in0=gate_f[:, cols], in1=c_raw[:, cols], op=ALU.mult)
 
         def fresh_half(k):
             cols = pair_cols((FIRST, LAST)[k])
-            nc.vector.tensor_tensor(out=fresh[:, cols], in0=gate_t[k][:], in1=gate_t[4 + k][:], op=ALU.mult)
-            backs[4 + k] = turn_back(fresh[:, cols], plain_psum, "plain")
+            nc.vector.tensor_tensor(out=fresh[:, cols], in0=gate_t[k][:], in1=gate_t[2 + k][:], op=ALU.mult)
 
-        def kept_half(k):
-            product(kept, c_raw, backs[2 + k], (FIRST, LAST)[k])
-
-        for s, (gate, tiles) in enumerate(units):
-            half = s % 2
-            bank = mx_product(gate, tiles)
-            ahead = (gate + 1, 1) if half == 0 else (gate + 2, 0)
-            if ahead[0] < GATES:
-                W[ahead] = new_grouped()
-                flip_w(ahead[0], ahead[1], 0, W[ahead], s_copy)
-            add_up(gate, bank, tiles[0])
-            if s >= 1:
-                std_of(s - 1)
-            add_up(gate, bank, tiles[1])
-            if s >= 1:
-                inverse_of(s - 1)
-                normalise(units[s - 1][0], units[s - 1][1], True)
-            squares_of(gate, tiles)
-            square_root(sum_squares[gate], roots[gate], tiles)
-            if ahead[0] < GATES:
-                flip_w(ahead[0], ahead[1], 1, W[ahead], s_copy)
-            if gate + 1 < GATES:
-                quantise_w(gate + 1, half, W[gate + 1, half])
-            if s < 3:
-                plain_product(1, 1 + s)
-            negated_mean(sums[gate], neg_means[gate], tiles)
-            if s >= 2:
-                turned[s - 2] = turn(units[s - 2][0], units[s - 2][1])
-                gate_t[s - 2] = activate(units[s - 2][0], FUNC[units[s - 2][0]], turned[s - 2])
-            if 4 <= s - 1 < 6:
-                backs[s - 3] = turn_back(gate_t[s - 3], plain_psum, "plain")
-            if s == 6:
-                kept_half(0)
-            if s == 7:
-                fresh_half(0)
-                kept_half(1)
-
-        late = flip_psum.tile([P, 2 * BANK], BF16, tag="flip")
-        spread_chunks(late[:, 0:UNITS], LNC_GAMMA_CHUNK, GATE_CHUNKS)
-        spread_chunks(late[:, UNITS : 2 * UNITS], LNC_BETA_CHUNK, GATE_CHUNKS)
-        lnc_gamma = late[:, 0:UNITS]
-        lnc_beta = late[:, UNITS : 2 * UNITS]
+        def fresh_back(k):
+            cols = pair_cols((FIRST, LAST)[k])
+            backs[k] = turn_back(fresh[:, cols], flip_psum, "flip")
 
         def cell_sum(t):
             nc.vector.scalar_tensor_tensor(
                 out=cell[:, block(t)],
-                in0=backs[4 + t // 2][:, (t % 2) * UNITS : (t % 2 + 1) * UNITS],
+                in0=backs[t // 2][:, (t % 2) * UNITS : (t % 2 + 1) * UNITS],
                 scalar=1.0,
                 in1=kept[:, block(t)],
                 op0=ALU.mult,
@@ -585,50 +620,129 @@ def tile_hyperlstmcell_pa_kernel(
             )
 
         def cell_square(tiles):
-            sum_of_squares(cell, sums[CELL], cell_squares, sum_squares[CELL], tiles)
+            squares = work.tile([P, BT * UNITS], F32, tag="squares")
+            sum_of_squares(cell, sums[CELL], squares, sum_squares[CELL], tiles)
             square_root(sum_squares[CELL], roots[CELL], tiles)
 
-        std_of(7)
-        fresh_half(1)
+        AHEAD = ((1, 1), (2, 0), (2, 1), (3, 0))
+        QUANTISED = ((1, 0), (1, 1), (2, 0), (2, 1), (3, 0))
+        for s in range(5):
+            position, tiles = units[s]
+            bank = mx_product(position, tiles)
+            if s < len(AHEAD):
+                flip_w_half(AHEAD[s][0], AHEAD[s][1], 0)
+            add_up(position, bank, tiles[0])
+            if s >= 1:
+                std_of(s - 1)
+            add_up(position, bank, tiles[1])
+            if s >= 1:
+                inverse_of(s - 1)
+            if 1 <= s < 4:
+                normalise_of(s - 1)
+            squares_and_root(s)
+            if s == 4:
+                normalise_of(3)
+            if s < len(AHEAD):
+                flip_w_half(AHEAD[s][0], AHEAD[s][1], 1)
+            quantise_w(QUANTISED[s][0], QUANTISED[s][1], W[QUANTISED[s]])
+            mean_of(s)
+            if s == 0:
+                plain_first_two(3)
+            if s in (1, 2):
+                plain_third((FIRST, LAST)[s - 1])
+            if s >= 2:
+                turn_and_activate(s - 2)
+
+        forget_centre(FIRST)
+        bank = mx_product(2, LAST)
+        flip_w_half(3, 1, 0)
+        flip_w_half(3, 1, 1)
+        fresh_half(0)
+        plain_last_matmuls(FIRST)
+        plain_last_matmuls(LAST)
+        fresh_back(0)
+        std_of(4)
+        add_up(2, bank, 2)
+        inverse_of(4)
+        add_up(2, bank, 3)
+        squares_and_root(5)
+        forget_finish(FIRST)
+        mean_of(5)
+        plain_last_copies(FIRST)
+        quantise_w(3, 1, W[3, 1])
+        turn_and_activate(3)
+        plain_last_copies(LAST)
+        bank_6 = mx_product(3, FIRST)
+        forget_centre(LAST)
+        bank_7 = mx_product(3, LAST)
+
+        kept_half(FIRST)
+        std_of(5)
         cell_sum(0)
-        inverse_of(7)
+        inverse_of(5)
         cell_sum(1)
         cell_square(FIRST)
-        normalise(units[7][0], units[7][1], True)
+        forget_finish(LAST)
+        fresh_half(1)
+        fresh_back(1)
         negated_mean(sums[CELL], neg_means[CELL], FIRST)
-        turned[6] = turn(3, FIRST)
-        gate_t[6] = activate(3, FUNC[3], turned[6])
+        add_up(3, bank_6, 0)
+        add_up(3, bank_6, 1)
+        kept_half(LAST)
+        mean_of(6)
+        squares_and_root(6)
         cell_sum(2)
         cell_sum(3)
         cell_square(LAST)
+        late = flip_psum.tile([P, 2 * BANK], BF16, tag="flip")
+        spread_chunks(late[:], [LNC_GAMMA_CHUNK + c for c in range(GATE_CHUNKS)] + [LNC_BETA_CHUNK + c for c in range(GATE_CHUNKS)])
+        lnc_gamma = late[:, 0:UNITS]
+        lnc_beta = late[:, UNITS : 2 * UNITS]
         centre(cell, neg_means[CELL], lnc_gamma, cell_centred, FIRST)
-        negated_mean(sums[CELL], neg_means[CELL], LAST)
-        turned[7] = turn(3, LAST)
-        gate_t[7] = activate(3, FUNC[3], turned[7])
         std_plus_eps(roots[CELL], std_epss[CELL], FIRST)
-        centre(cell, neg_means[CELL], lnc_gamma, cell_centred, range(2, 3))
+        negated_mean(sums[CELL], neg_means[CELL], LAST)
         inverse(std_epss[CELL], inv_stds[CELL], FIRST)
-        centre(cell, neg_means[CELL], lnc_gamma, cell_centred, range(3, 4))
-        scale_and_shift(cell_centred, inv_stds[CELL], lnc_beta, new_c, range(0, 1))
+        add_up(3, bank_7, 2)
+        std_of(6)
+        add_up(3, bank_7, 3)
+        inverse_of(6)
+        squares_and_root(7)
+        scale_and_shift(cell_centred, inv_stds[CELL], lnc_beta, new_c, FIRST)
+        mean_over_std(3, FIRST)
+        mean_of(7)
+        centre(cell, neg_means[CELL], lnc_gamma, cell_centred, range(2, 3))
+        normalise_of(6, False)
+        turned = [turn(3, FIRST)]
         std_plus_eps(roots[CELL], std_epss[CELL], LAST)
-        scale_and_shift(cell_centred, inv_stds[CELL], lnc_beta, new_c, range(1, 2))
+        centre(cell, neg_means[CELL], lnc_gamma, cell_centred, range(3, 4))
         inverse(std_epss[CELL], inv_stds[CELL], LAST)
-        gate_o = [turn_back(gate_t[6]), turn_back(gate_t[7])]
-
-        def finish(t):
-            nc.scalar.activation(out=tanh_c[:, block(t)], in_=new_c[:, block(t)], func=ACT.Tanh)
-            nc.vector.tensor_tensor(
-                out=new_h[:, block(t)],
-                in0=tanh_c[:, block(t)],
-                in1=gate_o[t // 2][:, (t % 2) * UNITS : (t % 2 + 1) * UNITS],
-                op=ALU.mult,
-            )
-
-        for t in FIRST:
-            nc.sync.dma_start(out=out_1_tiles[:, t, :], in_=new_c[:, block(t)])
+        std_of(7)
+        gate_t[6] = activate(3, ACT.Sigmoid, turned[0])
+        gate_o = [turn_back(gate_t[6], plain_psum, "plain")]
         scale_and_shift(cell_centred, inv_stds[CELL], lnc_beta, new_c, LAST)
-        for t in LAST:
-            nc.sync.dma_start(out=out_1_tiles[:, t, :], in_=new_c[:, block(t)])
-        for t in ALL:
-            finish(t)
-            nc.sync.dma_start(out=out_0_tiles[:, t, :], in_=new_h[:, block(t)])
+        inverse_of(7)
+        mean_over_std(3, LAST)
+        normalise_of(7, False)
+        turned.append(turn(3, LAST))
+
+        def tanh_of(tiles):
+            for t in tiles:
+                nc.sync.dma_start(out=out_1_tiles[:, t, :], in_=new_c[:, block(t)])
+                nc.scalar.activation(out=tanh_c[:, block(t)], in_=new_c[:, block(t)], func=ACT.Tanh)
+
+        def output_of(tiles):
+            for t in tiles:
+                nc.vector.tensor_tensor(
+                    out=new_h[:, block(t)],
+                    in0=tanh_c[:, block(t)],
+                    in1=gate_o[t // 2][:, (t % 2) * UNITS : (t % 2 + 1) * UNITS],
+                    op=ALU.mult,
+                )
+                nc.sync.dma_start(out=out_0_tiles[:, t, :], in_=new_h[:, block(t)])
+
+        tanh_of(FIRST)
+        gate_t[7] = activate(3, ACT.Sigmoid, turned[1])
+        gate_o.append(turn_back(gate_t[7], plain_psum, "plain"))
+        tanh_of(LAST)
+        output_of(FIRST)
+        output_of(LAST)

@@ -56,19 +56,16 @@ def tile_hyperlstmcell_pa_kernel(
         work = stack.enter_context(tc.tile_pool(name="work", bufs=2))
         small = stack.enter_context(tc.tile_pool(name="small", bufs=1))
         keep = stack.enter_context(tc.tile_pool(name="keep", bufs=1))
-        flip_psum = stack.enter_context(tc.psum_pool(name="flip_psum", bufs=4))
+        flip_psum = stack.enter_context(tc.psum_pool(name="flip_psum", bufs=3))
         mx_psum = stack.enter_context(tc.psum_pool(name="mx_psum", bufs=2))
         plain_psum = stack.enter_context(tc.psum_pool(name="plain_psum", bufs=2))
+        vector_psum = stack.enter_context(tc.psum_pool(name="vector_psum", bufs=1))
 
         def block(t):
             return slice(t * UNITS, (t + 1) * UNITS)
 
         norm_rows = consts.tile([P, P], BF16)
         nc.vector.memset(norm_rows[:], 0.0)
-        ones = consts.tile([P, P], BF16)
-        nc.vector.memset(ones[:], 1.0)
-        bias_row = consts.tile([P, UNITS], BF16)
-        nc.vector.memset(bias_row[:], 0.0)
         half_power = consts.tile([P, BT], F32)
         nc.vector.memset(half_power[:], 0.5)
         one_column = consts.tile([P, 1], F32)
@@ -113,9 +110,6 @@ def tile_hyperlstmcell_pa_kernel(
         nc.sync.dma_start(
             out=norm_rows[LNC_BETA_CHUNK : LNC_BETA_CHUNK + GATE_CHUNKS, :],
             in_=hc_lnc_beta.rearrange("(c q) -> c q", q=P),
-        )
-        nc.sync.dma_start(
-            out=bias_row[0:1, :], in_=hc_bih[OUTPUT * UNITS : (OUTPUT + 1) * UNITS].rearrange("(o n) -> o n", o=1)
         )
         nc.sync.dma_start(out=x_raw[:, half_cols[1]], in_=x_rows[:, half_cols[1]])
         nc.sync.dma_start(out=h_raw[:], in_=h.rearrange("(p t) k -> p (t k)", t=BT))
@@ -183,20 +177,19 @@ def tile_hyperlstmcell_pa_kernel(
             spread_chunks(bank[:], [chunk for gate in ORDER for chunk in gate_chunks(BIAS_CHUNK, gate)])
             nc.vector.tensor_copy(out=bias[:], in_=bank[:])
 
-        VECTOR_GATES = (FORGET,)
-        ln_vectors = consts.tile([P, BANK], BF16)
+        vectors = vector_psum.tile([P, 2 * BANK], BF16)
+        FORGET_GAMMA, FORGET_BETA, CELL_GAMMA, CELL_BETA = [
+            vectors[:, i * UNITS : (i + 1) * UNITS] for i in range(4)
+        ]
 
-        def spread_norm_vectors():
-            bank = flip_psum.tile([P, 2 * BANK], BF16, tag="flip")
+        def spread_vectors():
             spread_chunks(
-                bank[:],
-                [chunk for first in (GAMMA_CHUNK, BETA_CHUNK) for gate in VECTOR_GATES for chunk in gate_chunks(first, gate)],
+                vectors[:],
+                gate_chunks(GAMMA_CHUNK, FORGET)
+                + gate_chunks(BETA_CHUNK, FORGET)
+                + gate_chunks(LNC_GAMMA_CHUNK, 0)
+                + gate_chunks(LNC_BETA_CHUNK, 0),
             )
-            nc.vector.tensor_copy(out=ln_vectors[:], in_=bank[:, 0:BANK])
-
-        def gate_vector(which, position):
-            first = (which * len(VECTOR_GATES) + VECTOR_GATES.index(ORDER[position])) * UNITS
-            return ln_vectors[:, first : first + UNITS]
 
         plain = operands.tile([P, BT * N], F32)
 
@@ -204,48 +197,46 @@ def tile_hyperlstmcell_pa_kernel(
             first = t * N + position * UNITS
             return plain[:, first : first + UNITS]
 
-        def plain_matmuls(group, t, units, closed):
+        plain_banks = {}
+
+        def plain_matmuls(group, t, units):
             for step in range(KH):
                 nc.tensor.matmul(
                     out=group,
                     lhsT=hh_t[:, (step * BT + t) * P : (step * BT + t + 1) * P],
                     rhs=whh_t[:, step * N + units.start : step * N + units.stop],
                     start=(step == 0),
-                    stop=(step == KH - 1 and closed),
+                    stop=(step == KH - 1),
                 )
 
         def plain_first_two(t):
-            units = slice(0, BANK)
             bank = plain_psum.tile([P, BANK], F32, tag="plain")
-            plain_matmuls(bank[:], t, units, True)
+            plain_matmuls(bank[:], t, slice(0, BANK))
+            plain_banks[t] = bank
+
+        def plain_first_two_out(t):
             nc.vector.tensor_tensor(
-                out=plain[:, t * N : t * N + BANK], in0=bank[:], in1=bias[:, units], op=ALU.add
+                out=plain[:, t * N : t * N + BANK], in0=plain_banks[t][:], in1=bias[:, 0:BANK], op=ALU.add
             )
 
-        def plain_third(tiles):
-            units = slice(2 * UNITS, 3 * UNITS)
+
+        def plain_one(position, tiles):
+            units = slice(position * UNITS, (position + 1) * UNITS)
             bank = plain_psum.tile([P, BANK], F32, tag="plain")
             for i, t in enumerate(tiles):
-                plain_matmuls(bank[:, i * UNITS : (i + 1) * UNITS], t, units, True)
+                plain_matmuls(bank[:, i * UNITS : (i + 1) * UNITS], t, units)
+            plain_banks[position, tiles.start] = bank
+
+        def plain_one_out(position, tiles):
+            units = slice(position * UNITS, (position + 1) * UNITS)
+            bank = plain_banks[position, tiles.start]
             for i, t in enumerate(tiles):
                 nc.vector.tensor_tensor(
-                    out=plain_columns(2, t), in0=bank[:, i * UNITS : (i + 1) * UNITS], in1=bias[:, units], op=ALU.add
+                    out=plain_columns(position, t),
+                    in0=bank[:, i * UNITS : (i + 1) * UNITS],
+                    in1=bias[:, units],
+                    op=ALU.add,
                 )
-
-        last_banks = {}
-
-        def plain_last_matmuls(tiles):
-            units = slice(3 * UNITS, 4 * UNITS)
-            bank = plain_psum.tile([P, BANK], F32, tag="plain")
-            for i, t in enumerate(tiles):
-                group = bank[:, i * UNITS : (i + 1) * UNITS]
-                plain_matmuls(group, t, units, False)
-                nc.tensor.matmul(out=group, lhsT=ones[:], rhs=bias_row[:], start=False, stop=True)
-            last_banks[tiles.start] = bank
-
-        def plain_last_copies(tiles):
-            for i, t in enumerate(tiles):
-                nc.scalar.copy(out=plain_columns(3, t), in_=last_banks[tiles.start][:, i * UNITS : (i + 1) * UNITS])
 
         u_codes = operands.tile([P, PASSES * BATCH], U32, align_bytes=64)
         u_scales = operands.tile([P, PASSES * BATCH], U8, align_bytes=64)
@@ -348,13 +339,13 @@ def tile_hyperlstmcell_pa_kernel(
                     op1=ALU.mult,
                 )
 
-        def scale_and_shift(centred, inv_std, beta, out, tiles):
+        def shift(centred, std_eps, beta, tiles):
             for t in tiles:
                 nc.vector.scalar_tensor_tensor(
-                    out=out[:, block(t)],
-                    in0=centred[:, block(t)],
-                    scalar=inv_std[:, t : t + 1],
-                    in1=beta,
+                    out=centred[:, block(t)],
+                    in0=beta,
+                    scalar=std_eps[:, t : t + 1],
+                    in1=centred[:, block(t)],
                     op0=ALU.mult,
                     op1=ALU.add,
                 )
@@ -520,39 +511,13 @@ def tile_hyperlstmcell_pa_kernel(
         W = {}
         U = [new_grouped() for g in range(PASSES)]
 
-        def flip_w_half(position, i, b):
-            if b == 0:
-                W[position, i] = new_grouped()
-            flip_w(position, i, b, W[position, i], s_copy)
+        def flip_w_half(position, i):
+            W[position, i] = new_grouped()
+            for b in range(2):
+                flip_w(position, i, b, W[position, i], s_copy)
 
-        turn_hyper_h()
-        flip_u(0, 0, U[0], s_copy)
-        flip_u(1, 0, U[1], s_copy)
-        turn_whh(0)
-        turn_whh(1)
-        turn_norm_rows()
-        flip_u(0, 1, U[0], s_copy)
-        flip_u(1, 1, U[1], s_copy)
-        quantise_u(0, U[0])
-        quantise_u(1, U[1])
-        spread_bias()
-        plain_first_two(0)
-        for b in range(2):
-            flip_u(2, b, U[2], s_copy)
-            flip_u(3, b, U[3], s_copy)
-        flip_w_half(0, 0, 0)
-        flip_w_half(0, 0, 1)
-        plain_first_two(1)
-        quantise_u(2, U[2])
-        quantise_u(3, U[3])
-        flip_w_half(0, 1, 0)
-        flip_w_half(0, 1, 1)
-        quantise_w(0, 0, W[0, 0])
-        plain_first_two(2)
-        spread_norm_vectors()
-        flip_w_half(1, 0, 0)
-        flip_w_half(1, 0, 1)
-        quantise_w(0, 1, W[0, 1])
+        def quantise_w_half(position, i):
+            quantise_w(position, i, W[position, i])
 
         FUNC = (ACT.Sigmoid, ACT.Tanh, ACT.Sigmoid, ACT.Sigmoid)
         units = [(position, tiles) for position in range(GATES) for tiles in (FIRST, LAST)]
@@ -580,21 +545,35 @@ def tile_hyperlstmcell_pa_kernel(
             position, tiles = units[s]
             negated_mean(sums[position], neg_means[position], tiles)
 
-        def normalise_of(s, on_gpsimd=True):
-            normalise(units[s][0], units[s][1], on_gpsimd)
+        def normalise_of(s):
+            normalise(units[s][0], units[s][1], False)
 
-        def turn_and_activate(s):
-            position, tiles = units[s]
-            gate_t[s] = activate(position, FUNC[position], turn(position, tiles))
+        def ratio_of(s):
+            mean_over_std(units[s][0], units[s][1])
+
+        turned = {}
+
+        def turn_of(s):
+            turned[s] = turn(units[s][0], units[s][1])
+
+        def activate_of(s):
+            gate_t[s] = activate(units[s][0], FUNC[units[s][0]], turned[s])
 
         def forget_centre(tiles):
-            centre(vs[2], neg_means[2], gate_vector(0, 2), centred, tiles)
+            centre(vs[2], neg_means[2], FORGET_GAMMA, centred, tiles)
 
-        def forget_finish(tiles):
-            cols = pair_cols(tiles)
-            normed = work.tile([P, BT * UNITS], F32, tag="normed")
-            scale_and_shift(centred, inv_stds[2], gate_vector(1, 2), normed, tiles)
-            nc.scalar.activation(out=gate_f[:, cols], in_=normed[:, cols], func=ACT.Sigmoid, bias=one_column[:])
+        def forget_shift(tiles):
+            shift(centred, std_epss[2], FORGET_BETA, tiles)
+
+        def forget_activate(tiles):
+            for t in tiles:
+                nc.scalar.activation(
+                    out=gate_f[:, block(t)],
+                    in_=centred[:, block(t)],
+                    func=ACT.Sigmoid,
+                    scale=inv_stds[2][:, t : t + 1],
+                    bias=one_column[:],
+                )
 
         def kept_half(tiles):
             cols = pair_cols(tiles)
@@ -624,125 +603,216 @@ def tile_hyperlstmcell_pa_kernel(
             sum_of_squares(cell, sums[CELL], squares, sum_squares[CELL], tiles)
             square_root(sum_squares[CELL], roots[CELL], tiles)
 
-        AHEAD = ((1, 1), (2, 0), (2, 1), (3, 0))
-        QUANTISED = ((1, 0), (1, 1), (2, 0), (2, 1), (3, 0))
-        for s in range(5):
+        def cell_mean(tiles):
+            negated_mean(sums[CELL], neg_means[CELL], tiles)
+
+        def cell_centre(tiles):
+            centre(cell, neg_means[CELL], CELL_GAMMA, cell_centred, tiles)
+
+        def cell_std(tiles):
+            std_plus_eps(roots[CELL], std_epss[CELL], tiles)
+
+        def cell_inverse(tiles):
+            inverse(std_epss[CELL], inv_stds[CELL], tiles)
+
+        def cell_shift(tiles):
+            shift(cell_centred, std_epss[CELL], CELL_BETA, tiles)
+
+        def add_up_half(s, bank):
             position, tiles = units[s]
-            bank = mx_product(position, tiles)
-            if s < len(AHEAD):
-                flip_w_half(AHEAD[s][0], AHEAD[s][1], 0)
-            add_up(position, bank, tiles[0])
-            if s >= 1:
-                std_of(s - 1)
-            add_up(position, bank, tiles[1])
-            if s >= 1:
-                inverse_of(s - 1)
-            if 1 <= s < 4:
-                normalise_of(s - 1)
-            squares_and_root(s)
-            if s == 4:
-                normalise_of(3)
-            if s < len(AHEAD):
-                flip_w_half(AHEAD[s][0], AHEAD[s][1], 1)
-            quantise_w(QUANTISED[s][0], QUANTISED[s][1], W[QUANTISED[s]])
-            mean_of(s)
-            if s == 0:
-                plain_first_two(3)
-            if s in (1, 2):
-                plain_third((FIRST, LAST)[s - 1])
-            if s >= 2:
-                turn_and_activate(s - 2)
+            for t in tiles:
+                add_up(position, bank, t)
 
-        forget_centre(FIRST)
-        bank = mx_product(2, LAST)
-        flip_w_half(3, 1, 0)
-        flip_w_half(3, 1, 1)
-        fresh_half(0)
-        plain_last_matmuls(FIRST)
-        plain_last_matmuls(LAST)
-        fresh_back(0)
-        std_of(4)
-        add_up(2, bank, 2)
-        inverse_of(4)
-        add_up(2, bank, 3)
-        squares_and_root(5)
-        forget_finish(FIRST)
-        mean_of(5)
-        plain_last_copies(FIRST)
-        quantise_w(3, 1, W[3, 1])
-        turn_and_activate(3)
-        plain_last_copies(LAST)
-        bank_6 = mx_product(3, FIRST)
-        forget_centre(LAST)
-        bank_7 = mx_product(3, LAST)
+        def mx_half(s):
+            return mx_product(units[s][0], units[s][1])
 
-        kept_half(FIRST)
-        std_of(5)
-        cell_sum(0)
-        inverse_of(5)
-        cell_sum(1)
-        cell_square(FIRST)
-        forget_finish(LAST)
-        fresh_half(1)
-        fresh_back(1)
-        negated_mean(sums[CELL], neg_means[CELL], FIRST)
-        add_up(3, bank_6, 0)
-        add_up(3, bank_6, 1)
-        kept_half(LAST)
-        mean_of(6)
-        squares_and_root(6)
-        cell_sum(2)
-        cell_sum(3)
-        cell_square(LAST)
-        late = flip_psum.tile([P, 2 * BANK], BF16, tag="flip")
-        spread_chunks(late[:], [LNC_GAMMA_CHUNK + c for c in range(GATE_CHUNKS)] + [LNC_BETA_CHUNK + c for c in range(GATE_CHUNKS)])
-        lnc_gamma = late[:, 0:UNITS]
-        lnc_beta = late[:, UNITS : 2 * UNITS]
-        centre(cell, neg_means[CELL], lnc_gamma, cell_centred, FIRST)
-        std_plus_eps(roots[CELL], std_epss[CELL], FIRST)
-        negated_mean(sums[CELL], neg_means[CELL], LAST)
-        inverse(std_epss[CELL], inv_stds[CELL], FIRST)
-        add_up(3, bank_7, 2)
-        std_of(6)
-        add_up(3, bank_7, 3)
-        inverse_of(6)
-        squares_and_root(7)
-        scale_and_shift(cell_centred, inv_stds[CELL], lnc_beta, new_c, FIRST)
-        mean_over_std(3, FIRST)
-        mean_of(7)
-        centre(cell, neg_means[CELL], lnc_gamma, cell_centred, range(2, 3))
-        normalise_of(6, False)
-        turned = [turn(3, FIRST)]
-        std_plus_eps(roots[CELL], std_epss[CELL], LAST)
-        centre(cell, neg_means[CELL], lnc_gamma, cell_centred, range(3, 4))
-        inverse(std_epss[CELL], inv_stds[CELL], LAST)
-        std_of(7)
-        gate_t[6] = activate(3, ACT.Sigmoid, turned[0])
-        gate_o = [turn_back(gate_t[6], plain_psum, "plain")]
-        scale_and_shift(cell_centred, inv_stds[CELL], lnc_beta, new_c, LAST)
-        inverse_of(7)
-        mean_over_std(3, LAST)
-        normalise_of(7, False)
-        turned.append(turn(3, LAST))
+        def turn_back_of(s):
+            backs[s] = turn_back(gate_t[s], mx_psum, "mx")
 
         def tanh_of(tiles):
             for t in tiles:
+                nc.scalar.activation(
+                    out=tanh_c[:, block(t)],
+                    in_=cell_centred[:, block(t)],
+                    func=ACT.Tanh,
+                    scale=inv_stds[CELL][:, t : t + 1],
+                )
+
+        def new_c_of(tiles):
+            for t in tiles:
+                nc.vector.tensor_scalar_mul(
+                    out=new_c[:, block(t)], in0=cell_centred[:, block(t)], scalar1=inv_stds[CELL][:, t : t + 1]
+                )
                 nc.sync.dma_start(out=out_1_tiles[:, t, :], in_=new_c[:, block(t)])
-                nc.scalar.activation(out=tanh_c[:, block(t)], in_=new_c[:, block(t)], func=ACT.Tanh)
 
         def output_of(tiles):
             for t in tiles:
                 nc.vector.tensor_tensor(
                     out=new_h[:, block(t)],
                     in0=tanh_c[:, block(t)],
-                    in1=gate_o[t // 2][:, (t % 2) * UNITS : (t % 2 + 1) * UNITS],
+                    in1=backs[6 + t // 2][:, (t % 2) * UNITS : (t % 2 + 1) * UNITS],
                     op=ALU.mult,
                 )
                 nc.sync.dma_start(out=out_0_tiles[:, t, :], in_=new_h[:, block(t)])
 
+        turn_hyper_h()
+        flip_u(0, 0, U[0], s_copy)
+        flip_u(1, 0, U[1], s_copy)
+        turn_whh(0)
+        turn_whh(1)
+        turn_norm_rows()
+        flip_u(0, 1, U[0], s_copy)
+        flip_u(1, 1, U[1], s_copy)
+        plain_first_two(0)
+        quantise_u(0, U[0])
+        spread_bias()
+        quantise_u(1, U[1])
+        for b in range(2):
+            flip_u(2, b, U[2], s_copy)
+            flip_u(3, b, U[3], s_copy)
+        plain_first_two_out(0)
+        flip_w_half(0, 0)
+        quantise_u(2, U[2])
+        plain_first_two(1)
+        quantise_u(3, U[3])
+        flip_w_half(0, 1)
+        plain_first_two_out(1)
+        quantise_w_half(0, 0)
+        plain_first_two(2)
+        flip_w_half(1, 0)
+        quantise_w_half(0, 1)
+        plain_first_two_out(2)
+        plain_first_two(3)
+        flip_w_half(1, 1)
+        quantise_w_half(1, 0)
+
+        bank_0 = mx_half(0)
+        plain_first_two_out(3)
+        quantise_w_half(1, 1)
+        flip_w_half(2, 0)
+        bank_1 = mx_half(1)
+        add_up_half(0, bank_0)
+        squares_and_root(0)
+        mean_of(0)
+        flip_w_half(2, 1)
+        add_up_half(1, bank_1)
+        squares_and_root(1)
+        quantise_w_half(2, 0)
+        mean_of(1)
+        std_of(0)
+
+        bank_2 = mx_half(2)
+        inverse_of(0)
+        quantise_w_half(2, 1)
+        std_of(1)
+        ratio_of(0)
+        normalise_of(0)
+        bank_3 = mx_half(3)
+        add_up_half(2, bank_2)
+        inverse_of(1)
+        squares_and_root(2)
+        plain_one(2, FIRST)
+        flip_w_half(3, 0)
+        ratio_of(1)
+        add_up_half(3, bank_3)
+        plain_one_out(2, FIRST)
+        squares_and_root(3)
+        plain_one(2, LAST)
+        mean_of(2)
+        normalise_of(1)
+        std_of(2)
+        mean_of(3)
+
+        bank_4 = mx_half(4)
+        inverse_of(2)
+        quantise_w_half(3, 0)
+        plain_one_out(2, LAST)
+        ratio_of(2)
+        std_of(3)
+        bank_5 = mx_half(5)
+        normalise_of(2)
+        add_up_half(4, bank_4)
+        inverse_of(3)
+        squares_and_root(4)
+        mean_of(4)
+        flip_w_half(3, 1)
+        spread_vectors()
+        add_up_half(5, bank_5)
+        ratio_of(3)
+        squares_and_root(5)
+        forget_centre(FIRST)
+        mean_of(5)
+        turn_of(0)
+        turn_of(2)
+        normalise_of(3)
+        activate_of(0)
+        std_of(4)
+        forget_centre(LAST)
+        activate_of(2)
+        forget_shift(FIRST)
+        inverse_of(4)
+        quantise_w_half(3, 1)
+        std_of(5)
+        forget_activate(FIRST)
+        forget_shift(LAST)
+        inverse_of(5)
+        forget_activate(LAST)
+        plain_one(3, FIRST)
+        plain_one(3, LAST)
+        turn_of(1)
+        turn_of(3)
+        plain_one_out(3, FIRST)
+        bank_6 = mx_half(6)
+        bank_7 = mx_half(7)
+        fresh_half(0)
+        activate_of(1)
+        plain_one_out(3, LAST)
+        activate_of(3)
+        add_up_half(6, bank_6)
+        squares_and_root(6)
+        fresh_back(0)
+        kept_half(FIRST)
+        add_up_half(7, bank_7)
+        squares_and_root(7)
+        mean_of(6)
+        fresh_half(1)
+        fresh_back(1)
+        cell_sum(0)
+        cell_sum(1)
+        cell_square(FIRST)
+        std_of(6)
+        kept_half(LAST)
+        inverse_of(6)
+        mean_of(7)
+
+        cell_mean(FIRST)
+        ratio_of(6)
+        std_of(7)
+        cell_sum(2)
+        cell_sum(3)
+        normalise_of(6)
+        turn_of(6)
+        cell_square(LAST)
+        inverse_of(7)
+        cell_centre(FIRST)
+        ratio_of(7)
+        cell_mean(LAST)
+        cell_std(FIRST)
+        activate_of(6)
+        turn_back_of(6)
+        normalise_of(7)
+        turn_of(7)
+        cell_shift(FIRST)
+        cell_inverse(FIRST)
+        cell_centre(LAST)
         tanh_of(FIRST)
-        gate_t[7] = activate(3, ACT.Sigmoid, turned[1])
-        gate_o.append(turn_back(gate_t[7], plain_psum, "plain"))
-        tanh_of(LAST)
+        activate_of(7)
+        turn_back_of(7)
+        cell_std(LAST)
+        cell_shift(LAST)
+        cell_inverse(LAST)
+        new_c_of(FIRST)
         output_of(FIRST)
+        tanh_of(LAST)
+        new_c_of(LAST)
         output_of(LAST)

@@ -56,10 +56,9 @@ def tile_hyperlstmcell_pa_kernel(
         work = stack.enter_context(tc.tile_pool(name="work", bufs=2))
         small = stack.enter_context(tc.tile_pool(name="small", bufs=1))
         keep = stack.enter_context(tc.tile_pool(name="keep", bufs=1))
-        flip_psum = stack.enter_context(tc.psum_pool(name="flip_psum", bufs=3))
+        flip_psum = stack.enter_context(tc.psum_pool(name="flip_psum", bufs=4))
         mx_psum = stack.enter_context(tc.psum_pool(name="mx_psum", bufs=2))
         plain_psum = stack.enter_context(tc.psum_pool(name="plain_psum", bufs=2))
-        vector_psum = stack.enter_context(tc.psum_pool(name="vector_psum", bufs=1))
 
         def block(t):
             return slice(t * UNITS, (t + 1) * UNITS)
@@ -177,19 +176,20 @@ def tile_hyperlstmcell_pa_kernel(
             spread_chunks(bank[:], [chunk for gate in ORDER for chunk in gate_chunks(BIAS_CHUNK, gate)])
             nc.vector.tensor_copy(out=bias[:], in_=bank[:])
 
-        vectors = vector_psum.tile([P, 2 * BANK], BF16)
-        FORGET_GAMMA, FORGET_BETA, CELL_GAMMA, CELL_BETA = [
-            vectors[:, i * UNITS : (i + 1) * UNITS] for i in range(4)
-        ]
+        VECTOR_GATES = (FORGET,)
+        ln_vectors = consts.tile([P, BANK], BF16)
 
-        def spread_vectors():
+        def spread_norm_vectors():
+            bank = flip_psum.tile([P, 2 * BANK], BF16, tag="flip")
             spread_chunks(
-                vectors[:],
-                gate_chunks(GAMMA_CHUNK, FORGET)
-                + gate_chunks(BETA_CHUNK, FORGET)
-                + gate_chunks(LNC_GAMMA_CHUNK, 0)
-                + gate_chunks(LNC_BETA_CHUNK, 0),
+                bank[:],
+                [chunk for first in (GAMMA_CHUNK, BETA_CHUNK) for gate in VECTOR_GATES for chunk in gate_chunks(first, gate)],
             )
+            nc.vector.tensor_copy(out=ln_vectors[:], in_=bank[:, 0:BANK])
+
+        def gate_vector(which, position):
+            first = (which * len(VECTOR_GATES) + VECTOR_GATES.index(ORDER[position])) * UNITS
+            return ln_vectors[:, first : first + UNITS]
 
         plain = operands.tile([P, BT * N], F32)
 
@@ -560,10 +560,10 @@ def tile_hyperlstmcell_pa_kernel(
             gate_t[s] = activate(units[s][0], FUNC[units[s][0]], turned[s])
 
         def forget_centre(tiles):
-            centre(vs[2], neg_means[2], FORGET_GAMMA, centred, tiles)
+            centre(vs[2], neg_means[2], gate_vector(0, 2), centred, tiles)
 
         def forget_shift(tiles):
-            shift(centred, std_epss[2], FORGET_BETA, tiles)
+            shift(centred, std_epss[2], gate_vector(1, 2), tiles)
 
         def forget_activate(tiles):
             for t in tiles:
@@ -607,7 +607,7 @@ def tile_hyperlstmcell_pa_kernel(
             negated_mean(sums[CELL], neg_means[CELL], tiles)
 
         def cell_centre(tiles):
-            centre(cell, neg_means[CELL], CELL_GAMMA, cell_centred, tiles)
+            centre(cell, neg_means[CELL], cell_vectors[0], cell_centred, tiles)
 
         def cell_std(tiles):
             std_plus_eps(roots[CELL], std_epss[CELL], tiles)
@@ -616,7 +616,18 @@ def tile_hyperlstmcell_pa_kernel(
             inverse(std_epss[CELL], inv_stds[CELL], tiles)
 
         def cell_shift(tiles):
-            shift(cell_centred, std_epss[CELL], CELL_BETA, tiles)
+            shift(cell_centred, std_epss[CELL], cell_vectors[1], tiles)
+
+        cell_vectors = []
+
+        def spread_cell_vectors():
+            late = flip_psum.tile([P, 2 * BANK], BF16, tag="flip")
+            spread_chunks(
+                late[:],
+                [LNC_GAMMA_CHUNK + c for c in range(GATE_CHUNKS)] + [LNC_BETA_CHUNK + c for c in range(GATE_CHUNKS)],
+            )
+            cell_vectors.append(late[:, 0:UNITS])
+            cell_vectors.append(late[:, UNITS : 2 * UNITS])
 
         def add_up_half(s, bank):
             position, tiles = units[s]
@@ -627,7 +638,7 @@ def tile_hyperlstmcell_pa_kernel(
             return mx_product(units[s][0], units[s][1])
 
         def turn_back_of(s):
-            backs[s] = turn_back(gate_t[s], mx_psum, "mx")
+            backs[s] = turn_back(gate_t[s], plain_psum, "plain")
 
         def tanh_of(tiles):
             for t in tiles:
@@ -679,11 +690,12 @@ def tile_hyperlstmcell_pa_kernel(
         plain_first_two_out(1)
         quantise_w_half(0, 0)
         plain_first_two(2)
+        spread_norm_vectors()
         flip_w_half(1, 0)
         quantise_w_half(0, 1)
         plain_first_two_out(2)
-        plain_first_two(3)
         flip_w_half(1, 1)
+        plain_first_two(3)
         quantise_w_half(1, 0)
 
         bank_0 = mx_half(0)
@@ -736,7 +748,6 @@ def tile_hyperlstmcell_pa_kernel(
         squares_and_root(4)
         mean_of(4)
         flip_w_half(3, 1)
-        spread_vectors()
         add_up_half(5, bank_5)
         ratio_of(3)
         squares_and_root(5)
@@ -772,32 +783,33 @@ def tile_hyperlstmcell_pa_kernel(
         squares_and_root(6)
         fresh_back(0)
         kept_half(FIRST)
-        add_up_half(7, bank_7)
-        squares_and_root(7)
-        mean_of(6)
         fresh_half(1)
         fresh_back(1)
         cell_sum(0)
         cell_sum(1)
         cell_square(FIRST)
+        add_up_half(7, bank_7)
+        mean_of(6)
         std_of(6)
         kept_half(LAST)
+        squares_and_root(7)
         inverse_of(6)
-        mean_of(7)
 
-        cell_mean(FIRST)
+        spread_cell_vectors()
         ratio_of(6)
-        std_of(7)
         cell_sum(2)
         cell_sum(3)
         normalise_of(6)
         turn_of(6)
         cell_square(LAST)
-        inverse_of(7)
+        cell_mean(FIRST)
+        mean_of(7)
+        std_of(7)
         cell_centre(FIRST)
+        inverse_of(7)
+        cell_std(FIRST)
         ratio_of(7)
         cell_mean(LAST)
-        cell_std(FIRST)
         activate_of(6)
         turn_back_of(6)
         normalise_of(7)
@@ -805,14 +817,14 @@ def tile_hyperlstmcell_pa_kernel(
         cell_shift(FIRST)
         cell_inverse(FIRST)
         cell_centre(LAST)
+        cell_std(LAST)
         tanh_of(FIRST)
         activate_of(7)
         turn_back_of(7)
-        cell_std(LAST)
         cell_shift(LAST)
         cell_inverse(LAST)
+        tanh_of(LAST)
         new_c_of(FIRST)
         output_of(FIRST)
-        tanh_of(LAST)
         new_c_of(LAST)
         output_of(LAST)

@@ -421,12 +421,13 @@ def tile_hyperlstmcell_pa_kernel(
                         op1=ALU.mult,
                     )
                 else:
-                    nc.scalar.activation(
+                    nc.vector.tensor_scalar(
                         out=normeds[gate][:, block(t)],
-                        in_=vs[gate][:, block(t)],
-                        func=ACT.Identity,
-                        scale=inv_stds[gate][:, t : t + 1],
-                        bias=neg_mean_over_stds[gate][:, t : t + 1],
+                        in0=vs[gate][:, block(t)],
+                        scalar1=neg_means[gate][:, t : t + 1],
+                        scalar2=inv_stds[gate][:, t : t + 1],
+                        op0=ALU.add,
+                        op1=ALU.mult,
                     )
 
         neg_mean_over_stds = column_tiles("neg_mean_over_std")
@@ -651,8 +652,13 @@ def tile_hyperlstmcell_pa_kernel(
 
         def new_c_of(tiles):
             for t in tiles:
-                nc.vector.tensor_scalar_mul(
-                    out=new_c[:, block(t)], in0=cell_centred[:, block(t)], scalar1=inv_stds[CELL][:, t : t + 1]
+                nc.gpsimd.tensor_scalar(
+                    out=new_c[:, block(t)],
+                    in0=cell_centred[:, block(t)],
+                    scalar1=inv_stds[CELL][:, t : t + 1],
+                    scalar2=0.0,
+                    op0=ALU.mult,
+                    op1=ALU.add,
                 )
                 nc.sync.dma_start(out=out_1_tiles[:, t, :], in_=new_c[:, block(t)])
 
@@ -716,115 +722,110 @@ def tile_hyperlstmcell_pa_kernel(
         bank_2 = mx_half(2)
         inverse_of(0)
         quantise_w_half(2, 1)
-        std_of(1)
-        ratio_of(0)
         normalise_of(0)
         bank_3 = mx_half(3)
         add_up_half(2, bank_2)
-        inverse_of(1)
         squares_and_root(2)
         plain_one(2, FIRST)
         flip_w_half(3, 0)
-        ratio_of(1)
+        std_of(1)
         add_up_half(3, bank_3)
-        plain_one_out(2, FIRST)
+        inverse_of(1)
         squares_and_root(3)
         plain_one(2, LAST)
+        plain_one_out(2, FIRST)
         mean_of(2)
         normalise_of(1)
         std_of(2)
-        mean_of(3)
+        plain_one_out(2, LAST)
 
         bank_4 = mx_half(4)
         inverse_of(2)
         quantise_w_half(3, 0)
-        plain_one_out(2, LAST)
-        ratio_of(2)
-        std_of(3)
         bank_5 = mx_half(5)
-        normalise_of(2)
         add_up_half(4, bank_4)
-        inverse_of(3)
         squares_and_root(4)
-        mean_of(4)
-        flip_w_half(3, 1)
+        mean_of(3)
+        normalise_of(2)
         add_up_half(5, bank_5)
-        ratio_of(3)
+        flip_w_half(3, 1)
         squares_and_root(5)
-        forget_centre(FIRST)
-        mean_of(5)
+        mean_of(4)
+        std_of(3)
         turn_of(0)
         turn_of(2)
-        normalise_of(3)
-        activate_of(0)
-        std_of(4)
-        forget_centre(LAST)
-        activate_of(2)
-        forget_shift(FIRST)
-        inverse_of(4)
-        quantise_w_half(3, 1)
-        std_of(5)
-        forget_activate(FIRST)
-        forget_shift(LAST)
-        inverse_of(5)
-        forget_activate(LAST)
+        forget_centre(FIRST)
+        inverse_of(3)
+        mean_of(5)
         plain_one(3, FIRST)
         plain_one(3, LAST)
+        std_of(4)
+        normalise_of(3)
         turn_of(1)
         turn_of(3)
+        forget_shift(FIRST)
+        inverse_of(4)
+        forget_centre(LAST)
+        activate_of(0)
+        forget_activate(FIRST)
+        quantise_w_half(3, 1)
+        std_of(5)
+        activate_of(2)
         plain_one_out(3, FIRST)
+        forget_shift(LAST)
+        inverse_of(5)
+        activate_of(3)
+        forget_activate(LAST)
+        activate_of(1)
+
         bank_6 = mx_half(6)
         bank_7 = mx_half(7)
+        kept_half(FIRST)
         fresh_half(0)
-        activate_of(1)
+        fresh_back(0)
+        spread_cell_vectors()
         plain_one_out(3, LAST)
-        activate_of(3)
         add_up_half(6, bank_6)
         squares_and_root(6)
-        fresh_back(0)
-        kept_half(FIRST)
-        fresh_half(1)
-        fresh_back(1)
+        kept_half(LAST)
         cell_sum(0)
         cell_sum(1)
         cell_square(FIRST)
-        add_up_half(7, bank_7)
+        fresh_half(1)
+        fresh_back(1)
         mean_of(6)
         std_of(6)
-        kept_half(LAST)
-        squares_and_root(7)
+        add_up_half(7, bank_7)
         inverse_of(6)
-
-        spread_cell_vectors()
-        ratio_of(6)
-        cell_sum(2)
-        cell_sum(3)
+        squares_and_root(7)
+        cell_mean(FIRST)
         normalise_of(6)
         turn_of(6)
+        cell_sum(2)
+        cell_sum(3)
         cell_square(LAST)
-        cell_mean(FIRST)
-        mean_of(7)
-        std_of(7)
+
         cell_centre(FIRST)
-        inverse_of(7)
+        mean_of(7)
         cell_std(FIRST)
-        ratio_of(7)
-        cell_mean(LAST)
         activate_of(6)
         turn_back_of(6)
+        std_of(7)
+        cell_shift(FIRST)
+        inverse_of(7)
+        cell_inverse(FIRST)
+        cell_mean(LAST)
         normalise_of(7)
         turn_of(7)
-        cell_shift(FIRST)
-        cell_inverse(FIRST)
+        tanh_of(FIRST)
         cell_centre(LAST)
         cell_std(LAST)
-        tanh_of(FIRST)
         activate_of(7)
         turn_back_of(7)
+        new_c_of(FIRST)
         cell_shift(LAST)
         cell_inverse(LAST)
-        tanh_of(LAST)
-        new_c_of(FIRST)
         output_of(FIRST)
+        tanh_of(LAST)
         new_c_of(LAST)
         output_of(LAST)

@@ -65,6 +65,10 @@ def tile_hyperlstmcell_pa_kernel(
 
         norm_rows = consts.tile([P, P], BF16)
         nc.vector.memset(norm_rows[:], 0.0)
+        ones = consts.tile([P, P], BF16)
+        nc.vector.memset(ones[:], 1.0)
+        bias_row = consts.tile([P, BANK], BF16)
+        nc.vector.memset(bias_row[:], 0.0)
         half_power = consts.tile([P, BT], F32)
         nc.vector.memset(half_power[:], 0.5)
         one_column = consts.tile([P, 1], F32)
@@ -121,6 +125,12 @@ def tile_hyperlstmcell_pa_kernel(
                 in_=hc_Wih[gate * UNITS : (gate + 1) * UNITS, :].rearrange("(j p) k -> p j k", p=P),
             )
             w_raw.append(w_gate)
+            if position == 0:
+                for i, late_gate in enumerate(ORDER[2:]):
+                    nc.sync.dma_start(
+                        out=bias_row[0:1, i * UNITS : (i + 1) * UNITS],
+                        in_=hc_bih[late_gate * UNITS : (late_gate + 1) * UNITS].rearrange("(o n) -> o n", o=1),
+                    )
             if position == 1:
                 nc.sync.dma_start(out=c_raw[:], in_=hyper_c.rearrange("(p t) n -> p (t n)", t=BT))
 
@@ -199,14 +209,14 @@ def tile_hyperlstmcell_pa_kernel(
 
         plain_banks = {}
 
-        def plain_matmuls(group, t, units):
+        def plain_matmuls(group, t, units, closed=True):
             for step in range(KH):
                 nc.tensor.matmul(
                     out=group,
                     lhsT=hh_t[:, (step * BT + t) * P : (step * BT + t + 1) * P],
                     rhs=whh_t[:, step * N + units.start : step * N + units.stop],
                     start=(step == 0),
-                    stop=(step == KH - 1),
+                    stop=(step == KH - 1 and closed),
                 )
 
         def plain_first_two(t):
@@ -227,6 +237,23 @@ def tile_hyperlstmcell_pa_kernel(
                 plain_matmuls(bank[:, i * UNITS : (i + 1) * UNITS], t, units)
             plain_banks[position, tiles.start] = bank
 
+        def plain_late(position, tiles):
+            units = slice(position * UNITS, (position + 1) * UNITS)
+            bank = plain_psum.tile([P, BANK], F32, tag="plain")
+            for i, t in enumerate(tiles):
+                group = bank[:, i * UNITS : (i + 1) * UNITS]
+                plain_matmuls(group, t, units, False)
+                late_units = slice((position - 2) * UNITS, (position - 1) * UNITS)
+                nc.tensor.matmul(out=group, lhsT=ones[:], rhs=bias_row[:, late_units], start=False, stop=True)
+            plain_banks[position, tiles.start] = bank
+
+        def plain_late_out(position, tiles):
+            for i, t in enumerate(tiles):
+                nc.scalar.copy(
+                    out=plain_columns(position, t),
+                    in_=plain_banks[position, tiles.start][:, i * UNITS : (i + 1) * UNITS],
+                )
+
         def plain_one_out(position, tiles):
             units = slice(position * UNITS, (position + 1) * UNITS)
             bank = plain_banks[position, tiles.start]
@@ -245,6 +272,28 @@ def tile_hyperlstmcell_pa_kernel(
 
         X_WORDS = IN // 2
         ROW_WORDS = K // 2
+
+        sorted_pool = stack.enter_context(tc.tile_pool(name="sorted", bufs=2))
+        sorted_words = {}
+
+        def sort(key, raw, parts):
+            words = raw[:].bitcast(F32)
+            if key not in sorted_words:
+                result = sorted_pool.tile([P, 2 * ROW_WORDS], F32, tag="sorted")
+                sorted_words[key] = result
+            for part in parts:
+                cols = slice(part * ROW_WORDS, (part + 1) * ROW_WORDS)
+                nc.vector.tensor_copy(
+                    out=sorted_words[key][:, cols].rearrange("p (g u q) -> p g u q", u=2, q=P),
+                    in_=words[:, cols].rearrange("p (g q u) -> p g u q", u=2, q=P),
+                )
+
+        def word_view(key, raw, first):
+            if key in sorted_words:
+                words = sorted_words[key][:]
+                return lambda parity: words[:, first + parity * P : first + (parity + 1) * P]
+            words = raw[:].bitcast(F32)
+            return lambda parity: words[:, first + parity : first + PASS_WORDS : 2]
 
         def flip_piece(grouped, b, row_tiles, copy):
             grouped_words = grouped[:].bitcast(F32)
@@ -265,20 +314,15 @@ def tile_hyperlstmcell_pa_kernel(
             grouped = stage.tile([P, 2 * BANK * 2], BF16, align_bytes=64, tag="grouped")
             return grouped
 
-        def every_second(words, first):
-            return lambda parity: words[:, first + parity : first + PASS_WORDS : 2]
-
         def flip_u(g, b, grouped, copy):
             which, g_in = divmod(g, PASSES // 2)
             pair = (2 * b, 2 * b + 1)
-            words = (x_raw, h_raw)[which][:].bitcast(F32)
-            views = [every_second(words, t * X_WORDS + g_in * PASS_WORDS) for t in pair]
+            views = [word_view("xh"[which], (x_raw, h_raw)[which], t * X_WORDS + g_in * PASS_WORDS) for t in pair]
             flip_piece(grouped, b, views, copy)
 
         def flip_w(position, i, b, grouped, copy):
             g = 2 * i + b
-            words = w_raw[position][:].bitcast(F32)
-            views = [every_second(words, j * ROW_WORDS + g * PASS_WORDS) for j in range(2)]
+            views = [word_view(position, w_raw[position], j * ROW_WORDS + g * PASS_WORDS) for j in range(2)]
             flip_piece(grouped, b, views, copy)
 
         def quantise_u(g, grouped):
@@ -296,7 +340,9 @@ def tile_hyperlstmcell_pa_kernel(
 
         def negated_mean(sums, neg_mean, tiles):
             cols = cols_of(tiles)
-            nc.vector.tensor_scalar_mul(out=neg_mean[:, cols], in0=sums[:, cols], scalar1=-1.0 / UNITS)
+            nc.gpsimd.tensor_scalar(
+                out=neg_mean[:, cols], in0=sums[:, cols], scalar1=-1.0 / UNITS, scalar2=0.0, op0=ALU.mult, op1=ALU.add
+            )
 
         def sum_of_squares(values, sums, squares, sum_squares, tiles):
             for t in tiles:
@@ -540,6 +586,7 @@ def tile_hyperlstmcell_pa_kernel(
         def squares_and_root(s):
             position, tiles = units[s]
             squares_of(position, tiles)
+            negated_mean(sums[position], neg_means[position], tiles)
             square_root(sum_squares[position], roots[position], tiles)
 
         def mean_of(s):
@@ -602,6 +649,7 @@ def tile_hyperlstmcell_pa_kernel(
         def cell_square(tiles):
             squares = work.tile([P, BT * UNITS], F32, tag="squares")
             sum_of_squares(cell, sums[CELL], squares, sum_squares[CELL], tiles)
+            negated_mean(sums[CELL], neg_means[CELL], tiles)
             square_root(sum_squares[CELL], roots[CELL], tiles)
 
         def cell_mean(tiles):
@@ -694,6 +742,7 @@ def tile_hyperlstmcell_pa_kernel(
         quantise_u(3, U[3])
         flip_w_half(0, 1)
         plain_first_two_out(1)
+        sort(1, w_raw[1], range(2))
         quantise_w_half(0, 0)
         plain_first_two(2)
         spread_norm_vectors()
@@ -702,6 +751,7 @@ def tile_hyperlstmcell_pa_kernel(
         plain_first_two_out(2)
         flip_w_half(1, 1)
         plain_first_two(3)
+        sort(2, w_raw[2], range(2))
         quantise_w_half(1, 0)
 
         bank_0 = mx_half(0)
@@ -711,12 +761,10 @@ def tile_hyperlstmcell_pa_kernel(
         bank_1 = mx_half(1)
         add_up_half(0, bank_0)
         squares_and_root(0)
-        mean_of(0)
         flip_w_half(2, 1)
         add_up_half(1, bank_1)
         squares_and_root(1)
         quantise_w_half(2, 0)
-        mean_of(1)
         std_of(0)
 
         bank_2 = mx_half(2)
@@ -734,7 +782,6 @@ def tile_hyperlstmcell_pa_kernel(
         squares_and_root(3)
         plain_one(2, LAST)
         plain_one_out(2, FIRST)
-        mean_of(2)
         normalise_of(1)
         std_of(2)
         plain_one_out(2, LAST)
@@ -745,20 +792,17 @@ def tile_hyperlstmcell_pa_kernel(
         bank_5 = mx_half(5)
         add_up_half(4, bank_4)
         squares_and_root(4)
-        mean_of(3)
         normalise_of(2)
         add_up_half(5, bank_5)
         flip_w_half(3, 1)
         squares_and_root(5)
-        mean_of(4)
         std_of(3)
         turn_of(0)
         turn_of(2)
         forget_centre(FIRST)
         inverse_of(3)
-        mean_of(5)
-        plain_one(3, FIRST)
-        plain_one(3, LAST)
+        plain_late(3, FIRST)
+        plain_late(3, LAST)
         std_of(4)
         normalise_of(3)
         turn_of(1)
@@ -771,7 +815,7 @@ def tile_hyperlstmcell_pa_kernel(
         quantise_w_half(3, 1)
         std_of(5)
         activate_of(2)
-        plain_one_out(3, FIRST)
+        plain_late_out(3, FIRST)
         forget_shift(LAST)
         inverse_of(5)
         activate_of(3)
@@ -784,7 +828,7 @@ def tile_hyperlstmcell_pa_kernel(
         fresh_half(0)
         fresh_back(0)
         spread_cell_vectors()
-        plain_one_out(3, LAST)
+        plain_late_out(3, LAST)
         add_up_half(6, bank_6)
         squares_and_root(6)
         kept_half(LAST)
@@ -793,12 +837,10 @@ def tile_hyperlstmcell_pa_kernel(
         cell_square(FIRST)
         fresh_half(1)
         fresh_back(1)
-        mean_of(6)
         std_of(6)
         add_up_half(7, bank_7)
         inverse_of(6)
         squares_and_root(7)
-        cell_mean(FIRST)
         normalise_of(6)
         turn_of(6)
         cell_sum(2)
@@ -806,7 +848,6 @@ def tile_hyperlstmcell_pa_kernel(
         cell_square(LAST)
 
         cell_centre(FIRST)
-        mean_of(7)
         cell_std(FIRST)
         activate_of(6)
         turn_back_of(6)
@@ -814,7 +855,6 @@ def tile_hyperlstmcell_pa_kernel(
         cell_shift(FIRST)
         inverse_of(7)
         cell_inverse(FIRST)
-        cell_mean(LAST)
         normalise_of(7)
         turn_of(7)
         tanh_of(FIRST)

@@ -63,11 +63,13 @@ def tile_hyperlstmcell_pa_kernel(
         def block(t):
             return slice(t * UNITS, (t + 1) * UNITS)
 
+        bias_rows = consts.tile([P, P], BF16)
+        nc.vector.memset(bias_rows[:], 0.0)
         norm_rows = consts.tile([P, P], BF16)
         nc.vector.memset(norm_rows[:], 0.0)
         ones = consts.tile([P, P], BF16)
         nc.vector.memset(ones[:], 1.0)
-        bias_row = consts.tile([P, BANK], BF16)
+        bias_row = consts.tile([P, UNITS], BF16)
         nc.vector.memset(bias_row[:], 0.0)
         half_power = consts.tile([P, BT], F32)
         nc.vector.memset(half_power[:], 0.5)
@@ -84,8 +86,7 @@ def tile_hyperlstmcell_pa_kernel(
         ORDER = (INPUT, CELL_GATE, FORGET, OUTPUT)
 
         GATE_CHUNKS = UNITS // P
-        BIAS_CHUNK = 0
-        GAMMA_CHUNK = BIAS_CHUNK + N // P
+        GAMMA_CHUNK = 0
         BETA_CHUNK = GAMMA_CHUNK + N // P
         LNC_GAMMA_CHUNK = BETA_CHUNK + N // P
         LNC_BETA_CHUNK = LNC_GAMMA_CHUNK + GATE_CHUNKS
@@ -102,18 +103,7 @@ def tile_hyperlstmcell_pa_kernel(
             out=whh_raw[:].rearrange("p (j k) -> p j k", k=UNITS),
             in_=hc_Whh.rearrange("(j p) k -> p j k", p=P),
         )
-        nc.sync.dma_start(out=norm_rows[BIAS_CHUNK:GAMMA_CHUNK, :], in_=hc_bih.rearrange("(c q) -> c q", q=P))
-        nc.sync.dma_start(out=norm_rows[GAMMA_CHUNK:BETA_CHUNK, :], in_=hc_ln_gamma.rearrange("g (c q) -> (g c) q", q=P))
-        nc.sync.dma_start(
-            out=norm_rows[BETA_CHUNK:LNC_GAMMA_CHUNK, :], in_=hc_ln_beta.rearrange("g (c q) -> (g c) q", q=P)
-        )
-        nc.sync.dma_start(
-            out=norm_rows[LNC_GAMMA_CHUNK:LNC_BETA_CHUNK, :], in_=hc_lnc_gamma.rearrange("(c q) -> c q", q=P)
-        )
-        nc.sync.dma_start(
-            out=norm_rows[LNC_BETA_CHUNK : LNC_BETA_CHUNK + GATE_CHUNKS, :],
-            in_=hc_lnc_beta.rearrange("(c q) -> c q", q=P),
-        )
+        nc.sync.dma_start(out=bias_rows[0 : N // P, :], in_=hc_bih.rearrange("(c q) -> c q", q=P))
         nc.sync.dma_start(out=x_raw[:, half_cols[1]], in_=x_rows[:, half_cols[1]])
         nc.sync.dma_start(out=h_raw[:], in_=h.rearrange("(p t) k -> p (t k)", t=BT))
         c_raw = raw.tile([P, BT * UNITS], BF16)
@@ -125,12 +115,23 @@ def tile_hyperlstmcell_pa_kernel(
                 in_=hc_Wih[gate * UNITS : (gate + 1) * UNITS, :].rearrange("(j p) k -> p j k", p=P),
             )
             w_raw.append(w_gate)
-            if position == 0:
-                for i, late_gate in enumerate(ORDER[2:]):
-                    nc.sync.dma_start(
-                        out=bias_row[0:1, i * UNITS : (i + 1) * UNITS],
-                        in_=hc_bih[late_gate * UNITS : (late_gate + 1) * UNITS].rearrange("(o n) -> o n", o=1),
-                    )
+            if position == 1:
+                nc.sync.dma_start(
+                    out=norm_rows[GAMMA_CHUNK:BETA_CHUNK, :], in_=hc_ln_gamma.rearrange("g (c q) -> (g c) q", q=P)
+                )
+                nc.sync.dma_start(
+                    out=norm_rows[BETA_CHUNK:LNC_GAMMA_CHUNK, :], in_=hc_ln_beta.rearrange("g (c q) -> (g c) q", q=P)
+                )
+                nc.sync.dma_start(
+                    out=norm_rows[LNC_GAMMA_CHUNK:LNC_BETA_CHUNK, :], in_=hc_lnc_gamma.rearrange("(c q) -> c q", q=P)
+                )
+                nc.sync.dma_start(
+                    out=norm_rows[LNC_BETA_CHUNK : LNC_BETA_CHUNK + GATE_CHUNKS, :],
+                    in_=hc_lnc_beta.rearrange("(c q) -> c q", q=P),
+                )
+                nc.sync.dma_start(
+                    out=bias_row[0:1, :], in_=hc_bih[OUTPUT * UNITS : (OUTPUT + 1) * UNITS].rearrange("(o n) -> o n", o=1)
+                )
             if position == 1:
                 nc.sync.dma_start(out=c_raw[:], in_=hyper_c.rearrange("(p t) n -> p (t n)", t=BT))
 
@@ -159,8 +160,14 @@ def tile_hyperlstmcell_pa_kernel(
                 )
             nc.scalar.copy(out=whh_t[:, step * N : (step + 1) * N], in_=bank[:])
 
+        bias_cols = consts.tile([P, P], BF16)
         norm_cols = consts.tile([P, P], BF16)
         norm_cols_f32 = consts.tile([P, P], F32)
+
+        def turn_bias_rows():
+            bank = flip_psum.tile([P, 2 * BANK], BF16, tag="flip")
+            nc.tensor.transpose(out=bank[:, 0:P], in_=bias_rows[:], identity=ident_bf16[:])
+            nc.vector.tensor_copy(out=bias_cols[:], in_=bank[:, 0:P])
 
         def turn_norm_rows():
             bank = flip_psum.tile([P, 2 * BANK], BF16, tag="flip")
@@ -168,11 +175,11 @@ def tile_hyperlstmcell_pa_kernel(
             nc.vector.tensor_copy(out=norm_cols[:], in_=bank[:, 0:P])
             nc.vector.tensor_copy(out=norm_cols_f32[:], in_=bank[:, 0:P])
 
-        def spread_chunks(bank, chunks):
+        def spread_chunks(bank, columns, chunks):
             for i, chunk in enumerate(chunks):
                 nc.tensor.transpose(
                     out=bank[:, i * P : (i + 1) * P],
-                    in_=norm_cols[:, chunk : chunk + 1].to_broadcast([P, P]),
+                    in_=columns[:, chunk : chunk + 1].to_broadcast([P, P]),
                     identity=ident_bf16[:],
                 )
 
@@ -183,7 +190,7 @@ def tile_hyperlstmcell_pa_kernel(
 
         def spread_bias():
             bank = flip_psum.tile([P, 2 * BANK], BF16, tag="flip")
-            spread_chunks(bank[:], [chunk for gate in ORDER for chunk in gate_chunks(BIAS_CHUNK, gate)])
+            spread_chunks(bank[:], bias_cols, [chunk for gate in ORDER for chunk in gate_chunks(0, gate)])
             nc.vector.tensor_copy(out=bias[:], in_=bank[:])
 
         VECTOR_GATES = (FORGET,)
@@ -193,6 +200,7 @@ def tile_hyperlstmcell_pa_kernel(
             bank = flip_psum.tile([P, 2 * BANK], BF16, tag="flip")
             spread_chunks(
                 bank[:],
+                norm_cols,
                 [chunk for first in (GAMMA_CHUNK, BETA_CHUNK) for gate in VECTOR_GATES for chunk in gate_chunks(first, gate)],
             )
             nc.vector.tensor_copy(out=ln_vectors[:], in_=bank[:, 0:BANK])
@@ -243,8 +251,7 @@ def tile_hyperlstmcell_pa_kernel(
             for i, t in enumerate(tiles):
                 group = bank[:, i * UNITS : (i + 1) * UNITS]
                 plain_matmuls(group, t, units, False)
-                late_units = slice((position - 2) * UNITS, (position - 1) * UNITS)
-                nc.tensor.matmul(out=group, lhsT=ones[:], rhs=bias_row[:, late_units], start=False, stop=True)
+                nc.tensor.matmul(out=group, lhsT=ones[:], rhs=bias_row[:], start=False, stop=True)
             plain_banks[position, tiles.start] = bank
 
         def plain_late_out(position, tiles):
@@ -673,6 +680,7 @@ def tile_hyperlstmcell_pa_kernel(
             late = flip_psum.tile([P, 2 * BANK], BF16, tag="flip")
             spread_chunks(
                 late[:],
+                norm_cols,
                 [LNC_GAMMA_CHUNK + c for c in range(GATE_CHUNKS)] + [LNC_BETA_CHUNK + c for c in range(GATE_CHUNKS)],
             )
             cell_vectors.append(late[:, 0:UNITS])
@@ -725,7 +733,7 @@ def tile_hyperlstmcell_pa_kernel(
         flip_u(1, 0, U[1], s_copy)
         turn_whh(0)
         turn_whh(1)
-        turn_norm_rows()
+        turn_bias_rows()
         flip_u(0, 1, U[0], s_copy)
         flip_u(1, 1, U[1], s_copy)
         plain_first_two(0)
@@ -745,7 +753,6 @@ def tile_hyperlstmcell_pa_kernel(
         sort(1, w_raw[1], range(2))
         quantise_w_half(0, 0)
         plain_first_two(2)
-        spread_norm_vectors()
         flip_w_half(1, 0)
         quantise_w_half(0, 1)
         plain_first_two_out(2)
@@ -767,6 +774,7 @@ def tile_hyperlstmcell_pa_kernel(
         quantise_w_half(2, 0)
         std_of(0)
 
+        turn_norm_rows()
         bank_2 = mx_half(2)
         inverse_of(0)
         quantise_w_half(2, 1)
@@ -786,6 +794,7 @@ def tile_hyperlstmcell_pa_kernel(
         std_of(2)
         plain_one_out(2, LAST)
 
+        spread_norm_vectors()
         bank_4 = mx_half(4)
         inverse_of(2)
         quantise_w_half(3, 0)
@@ -837,8 +846,8 @@ def tile_hyperlstmcell_pa_kernel(
         cell_square(FIRST)
         fresh_half(1)
         fresh_back(1)
-        std_of(6)
         add_up_half(7, bank_7)
+        std_of(6)
         inverse_of(6)
         squares_and_root(7)
         normalise_of(6)

import math
from contextlib import ExitStack

import concourse.mybir as mybir
from concourse.masks import make_identity

F32 = mybir.dt.float32
BF16 = mybir.dt.bfloat16
U32 = mybir.dt.uint32
U8 = mybir.dt.uint8
FP8X4 = mybir.dt.float8_e4m3fn_x4
ALU = mybir.AluOpType
ACT = mybir.ActivationFunctionType

P = 128
BATCH = 512
BT = BATCH // P
IN = 1024
K = 2 * IN
UNITS = 256
GATES = 4
N = GATES * UNITS
KH = UNITS // P
K_PASS = 4 * P
PASSES = K // K_PASS
PASS_WORDS = K_PASS // 2
BANK = 512
EPS = 1e-6

FLOPS = 2 * BATCH * N * K + 2 * BATCH * N * UNITS


def tile_hyperlstmcell_pa_kernel(
    tc,
    x,
    h,
    hyper_h,
    hyper_c,
    hc_Wih,
    hc_bih,
    hc_Whh,
    hc_ln_gamma,
    hc_ln_beta,
    hc_lnc_gamma,
    hc_lnc_beta,
    out_0,
    out_1,
):
    nc = tc.nc
    with ExitStack() as stack:
        stack.enter_context(tc.manual_schedule())
        consts = stack.enter_context(tc.tile_pool(name="consts", bufs=1))
        raw = stack.enter_context(tc.tile_pool(name="raw", bufs=1))
        operands = stack.enter_context(tc.tile_pool(name="operands", bufs=1))
        stage = stack.enter_context(tc.tile_pool(name="stage", bufs=4))
        work = stack.enter_context(tc.tile_pool(name="work", bufs=2))
        small = stack.enter_context(tc.tile_pool(name="small", bufs=1))
        keep = stack.enter_context(tc.tile_pool(name="keep", bufs=1))
        flip_psum = stack.enter_context(tc.psum_pool(name="flip_psum", bufs=4))
        mx_psum = stack.enter_context(tc.psum_pool(name="mx_psum", bufs=2))
        plain_psum = stack.enter_context(tc.psum_pool(name="plain_psum", bufs=2))

        def block(t):
            return slice(t * UNITS, (t + 1) * UNITS)

        bias_rows = consts.tile([P, P], BF16)
        nc.vector.memset(bias_rows[:], 0.0)
        norm_rows = consts.tile([P, P], BF16)
        nc.vector.memset(norm_rows[:], 0.0)
        ones = consts.tile([P, P], BF16)
        nc.vector.memset(ones[:], 1.0)
        bias_row = consts.tile([P, UNITS], BF16)
        nc.vector.memset(bias_row[:], 0.0)
        half_power = consts.tile([P, BT], F32)
        nc.vector.memset(half_power[:], 0.5)
        one_column = consts.tile([P, 1], F32)
        nc.vector.memset(one_column[:], 1.0)
        ident_bf16 = consts.tile([P, P], BF16)
        make_identity(nc, ident_bf16[:])
        ident_f32 = consts.tile([P, P], F32)
        make_identity(nc, ident_f32[:])
        table_warmer = consts.tile([P, 1], F32)
        nc.scalar.activation(out=table_warmer[:], in_=one_column[:], func=ACT.Sigmoid)

        INPUT, FORGET, CELL_GATE, OUTPUT = range(GATES)
        ORDER = (INPUT, CELL_GATE, FORGET, OUTPUT)

        GATE_CHUNKS = UNITS // P
        GAMMA_CHUNK = 0
        BETA_CHUNK = GAMMA_CHUNK + N // P
        LNC_GAMMA_CHUNK = BETA_CHUNK + N // P
        LNC_BETA_CHUNK = LNC_GAMMA_CHUNK + GATE_CHUNKS

        hh_raw = raw.tile([P, BT * UNITS], BF16)
        nc.sync.dma_start(out=hh_raw[:], in_=hyper_h.rearrange("(p t) k -> p (t k)", t=BT))
        x_raw = raw.tile([P, BT * IN], BF16)
        h_raw = raw.tile([P, BT * IN], BF16)
        half_cols = (slice(0, BT // 2 * IN), slice(BT // 2 * IN, BT * IN))
        x_rows = x.rearrange("(p t) k -> p (t k)", t=BT)
        nc.sync.dma_start(out=x_raw[:, half_cols[0]], in_=x_rows[:, half_cols[0]])
        whh_raw = raw.tile([P, (N // P) * UNITS], BF16)
        nc.sync.dma_start(
            out=whh_raw[:].rearrange("p (j k) -> p j k", k=UNITS),
            in_=hc_Whh.rearrange("(j p) k -> p j k", p=P),
        )
        nc.sync.dma_start(out=bias_rows[0 : N // P, :], in_=hc_bih.rearrange("(c q) -> c q", q=P))
        nc.sync.dma_start(out=x_raw[:, half_cols[1]], in_=x_rows[:, half_cols[1]])
        nc.sync.dma_start(out=h_raw[:], in_=h.rearrange("(p t) k -> p (t k)", t=BT))
        c_raw = raw.tile([P, BT * UNITS], BF16)
        w_raw = []
        for position, gate in enumerate(ORDER):
            w_gate = raw.tile([P, 2 * K], BF16, name="w_raw%d" % position)
            nc.sync.dma_start(
                out=w_gate[:].rearrange("p (j k) -> p j k", k=K),
                in_=hc_Wih[gate * UNITS : (gate + 1) * UNITS, :].rearrange("(j p) k -> p j k", p=P),
            )
            w_raw.append(w_gate)
            if position == 1:
                nc.sync.dma_start(
                    out=norm_rows[GAMMA_CHUNK:BETA_CHUNK, :], in_=hc_ln_gamma.rearrange("g (c q) -> (g c) q", q=P)
                )
                nc.sync.dma_start(
                    out=norm_rows[BETA_CHUNK:LNC_GAMMA_CHUNK, :], in_=hc_ln_beta.rearrange("g (c q) -> (g c) q", q=P)
                )
                nc.sync.dma_start(
                    out=norm_rows[LNC_GAMMA_CHUNK:LNC_BETA_CHUNK, :], in_=hc_lnc_gamma.rearrange("(c q) -> c q", q=P)
                )
                nc.sync.dma_start(
                    out=norm_rows[LNC_BETA_CHUNK : LNC_BETA_CHUNK + GATE_CHUNKS, :],
                    in_=hc_lnc_beta.rearrange("(c q) -> c q", q=P),
                )
                nc.sync.dma_start(
                    out=bias_row[0:1, :], in_=hc_bih[OUTPUT * UNITS : (OUTPUT + 1) * UNITS].rearrange("(o n) -> o n", o=1)
                )
            if position == 1:
                nc.sync.dma_start(out=c_raw[:], in_=hyper_c.rearrange("(p t) n -> p (t n)", t=BT))

        hh_t = operands.tile([P, KH * BT * P], BF16)
        whh_t = operands.tile([P, KH * N], BF16)

        def turn_hyper_h():
            bank = flip_psum.tile([P, 2 * BANK], BF16, tag="flip")
            for step in range(KH):
                for t in range(BT):
                    nc.tensor.transpose(
                        out=bank[:, (step * BT + t) * P : (step * BT + t + 1) * P],
                        in_=hh_raw[:, t * UNITS + step * P : t * UNITS + (step + 1) * P],
                        identity=ident_bf16[:],
                    )
            nc.scalar.copy(out=hh_t[:], in_=bank[:])

        def turn_whh(step):
            bank = flip_psum.tile([P, 2 * BANK], BF16, tag="flip")
            for slot in range(N // P):
                j = ORDER[slot // GATE_CHUNKS] * GATE_CHUNKS + slot % GATE_CHUNKS
                nc.tensor.transpose(
                    out=bank[:, slot * P : (slot + 1) * P],
                    in_=whh_raw[:, j * UNITS + step * P : j * UNITS + (step + 1) * P],
                    identity=ident_bf16[:],
                )
            nc.scalar.copy(out=whh_t[:, step * N : (step + 1) * N], in_=bank[:])

        bias_cols = consts.tile([P, P], BF16)
        norm_cols = consts.tile([P, P], BF16)
        norm_cols_f32 = consts.tile([P, P], F32)

        def turn_bias_rows():
            bank = flip_psum.tile([P, 2 * BANK], BF16, tag="flip")
            nc.tensor.transpose(out=bank[:, 0:P], in_=bias_rows[:], identity=ident_bf16[:])
            nc.vector.tensor_copy(out=bias_cols[:], in_=bank[:, 0:P])

        def turn_norm_rows():
            bank = flip_psum.tile([P, 2 * BANK], BF16, tag="flip")
            nc.tensor.transpose(out=bank[:, 0:P], in_=norm_rows[:], identity=ident_bf16[:])
            nc.vector.tensor_copy(out=norm_cols[:], in_=bank[:, 0:P])
            nc.vector.tensor_copy(out=norm_cols_f32[:], in_=bank[:, 0:P])

        def spread_chunks(bank, columns, chunks):
            for i, chunk in enumerate(chunks):
                nc.tensor.transpose(
                    out=bank[:, i * P : (i + 1) * P],
                    in_=columns[:, chunk : chunk + 1].to_broadcast([P, P]),
                    identity=ident_bf16[:],
                )

        def gate_chunks(first, gate):
            return [first + gate * GATE_CHUNKS + c for c in range(GATE_CHUNKS)]

        bias = consts.tile([P, N], BF16)

        def spread_bias():
            bank = flip_psum.tile([P, 2 * BANK], BF16, tag="flip")
            spread_chunks(bank[:], bias_cols, [chunk for gate in ORDER for chunk in gate_chunks(0, gate)])
            nc.vector.tensor_copy(out=bias[:], in_=bank[:])

        VECTOR_GATES = (FORGET,)
        ln_vectors = consts.tile([P, BANK], BF16)

        def spread_norm_vectors():
            bank = flip_psum.tile([P, 2 * BANK], BF16, tag="flip")
            spread_chunks(
                bank[:],
                norm_cols,
                [chunk for first in (GAMMA_CHUNK, BETA_CHUNK) for gate in VECTOR_GATES for chunk in gate_chunks(first, gate)],
            )
            nc.vector.tensor_copy(out=ln_vectors[:], in_=bank[:, 0:BANK])

        def gate_vector(which, position):
            first = (which * len(VECTOR_GATES) + VECTOR_GATES.index(ORDER[position])) * UNITS
            return ln_vectors[:, first : first + UNITS]

        plain = operands.tile([P, BT * N], F32)

        def plain_columns(position, t):
            first = t * N + position * UNITS
            return plain[:, first : first + UNITS]

        plain_banks = {}

        def plain_matmuls(group, t, units, closed=True):
            for step in range(KH):
                nc.tensor.matmul(
                    out=group,
                    lhsT=hh_t[:, (step * BT + t) * P : (step * BT + t + 1) * P],
                    rhs=whh_t[:, step * N + units.start : step * N + units.stop],
                    start=(step == 0),
                    stop=(step == KH - 1 and closed),
                )

        def plain_first_two(t):
            bank = plain_psum.tile([P, BANK], F32, tag="plain")
            plain_matmuls(bank[:], t, slice(0, BANK))
            plain_banks[t] = bank

        def plain_first_two_out(t):
            nc.vector.tensor_tensor(
                out=plain[:, t * N : t * N + BANK], in0=plain_banks[t][:], in1=bias[:, 0:BANK], op=ALU.add
            )


        def plain_one(position, tiles):
            units = slice(position * UNITS, (position + 1) * UNITS)
            bank = plain_psum.tile([P, BANK], F32, tag="plain")
            for i, t in enumerate(tiles):
                plain_matmuls(bank[:, i * UNITS : (i + 1) * UNITS], t, units)
            plain_banks[position, tiles.start] = bank

        def plain_late(position, tiles):
            units = slice(position * UNITS, (position + 1) * UNITS)
            bank = plain_psum.tile([P, BANK], F32, tag="plain")
            for i, t in enumerate(tiles):
                group = bank[:, i * UNITS : (i + 1) * UNITS]
                plain_matmuls(group, t, units, False)
                nc.tensor.matmul(out=group, lhsT=ones[:], rhs=bias_row[:], start=False, stop=True)
            plain_banks[position, tiles.start] = bank

        def plain_late_out(position, tiles):
            for i, t in enumerate(tiles):
                nc.scalar.copy(
                    out=plain_columns(position, t),
                    in_=plain_banks[position, tiles.start][:, i * UNITS : (i + 1) * UNITS],
                )

        def plain_one_out(position, tiles):
            units = slice(position * UNITS, (position + 1) * UNITS)
            bank = plain_banks[position, tiles.start]
            for i, t in enumerate(tiles):
                nc.vector.tensor_tensor(
                    out=plain_columns(position, t),
                    in0=bank[:, i * UNITS : (i + 1) * UNITS],
                    in1=bias[:, units],
                    op=ALU.add,
                )

        u_codes = operands.tile([P, PASSES * BATCH], U32, align_bytes=64)
        u_scales = operands.tile([P, PASSES * BATCH], U8, align_bytes=64)
        w_codes = operands.tile([P, GATES * PASSES * UNITS], U32, align_bytes=64)
        w_scales = operands.tile([P, GATES * PASSES * UNITS], U8, align_bytes=64)

        X_WORDS = IN // 2
        ROW_WORDS = K // 2

        sorted_pool = stack.enter_context(tc.tile_pool(name="sorted", bufs=2))
        sorted_words = {}

        def sort(key, raw, parts):
            words = raw[:].bitcast(F32)
            if key not in sorted_words:
                result = sorted_pool.tile([P, 2 * ROW_WORDS], F32, tag="sorted")
                sorted_words[key] = result
            for part in parts:
                cols = slice(part * ROW_WORDS, (part + 1) * ROW_WORDS)
                nc.vector.tensor_copy(
                    out=sorted_words[key][:, cols].rearrange("p (g u q) -> p g u q", u=2, q=P),
                    in_=words[:, cols].rearrange("p (g q u) -> p g u q", u=2, q=P),
                )

        def word_view(key, raw, first):
            if key in sorted_words:
                words = sorted_words[key][:]
                return lambda parity: words[:, first + parity * P : first + (parity + 1) * P]
            words = raw[:].bitcast(F32)
            return lambda parity: words[:, first + parity : first + PASS_WORDS : 2]

        def flip_piece(grouped, b, row_tiles, copy):
            grouped_words = grouped[:].bitcast(F32)
            bank = flip_psum.tile([P, BANK], F32, tag="flip")
            for parity in range(2):
                for i in range(2):
                    nc.tensor.transpose(
                        out=bank[:, (2 * parity + i) * P : (2 * parity + i + 1) * P],
                        in_=row_tiles[i](parity),
                        identity=ident_f32[:],
                    )
            copy(
                out=grouped_words[:, b * BANK : (b + 1) * BANK].rearrange("p (r u) -> p r u", u=2),
                in_=bank[:].rearrange("p (u r) -> p r u", u=2),
            )

        def new_grouped():
            grouped = stage.tile([P, 2 * BANK * 2], BF16, align_bytes=64, tag="grouped")
            return grouped

        def flip_u(g, b, grouped, copy):
            which, g_in = divmod(g, PASSES // 2)
            pair = (2 * b, 2 * b + 1)
            views = [word_view("xh"[which], (x_raw, h_raw)[which], t * X_WORDS + g_in * PASS_WORDS) for t in pair]
            flip_piece(grouped, b, views, copy)

        def flip_w(position, i, b, grouped, copy):
            g = 2 * i + b
            views = [word_view(position, w_raw[position], j * ROW_WORDS + g * PASS_WORDS) for j in range(2)]
            flip_piece(grouped, b, views, copy)

        def quantise_u(g, grouped):
            cols = slice(g * BATCH, (g + 1) * BATCH)
            nc.vector.quantize_mx(out=u_codes[:, cols].bitcast(FP8X4), scales=u_scales[:, cols], in_=grouped[:])

        def quantise_w(gate, i, grouped):
            first = (gate * PASSES + 2 * i) * UNITS
            cols = slice(first, first + 2 * UNITS)
            nc.vector.quantize_mx(out=w_codes[:, cols].bitcast(FP8X4), scales=w_scales[:, cols], in_=grouped[:])

        def cols_of(tiles):
            return slice(tiles.start, tiles.stop)


        def negated_mean(sums, neg_mean, tiles):
            cols = cols_of(tiles)
            nc.gpsimd.tensor_scalar(
                out=neg_mean[:, cols], in0=sums[:, cols], scalar1=-1.0 / UNITS, scalar2=0.0, op0=ALU.mult, op1=ALU.add
            )

        def sum_of_squares(values, sums, squares, sum_squares, tiles):
            for t in tiles:
                nc.scalar.activation(
                    out=squares[:, block(t)],
                    in_=values[:, block(t)],
                    func=ACT.Square,
                    scale=-float(UNITS),
                    bias=sums[:, t : t + 1],
                    accum_out=sum_squares[:, t : t + 1],
                )

        def square_root(sum_squares, root, tiles):
            cols = cols_of(tiles)
            nc.gpsimd.tensor_tensor(out=root[:, cols], in0=sum_squares[:, cols], in1=half_power[:, cols], op=ALU.pow)

        def std_plus_eps(root, std_eps, tiles):
            cols = cols_of(tiles)
            nc.vector.tensor_scalar(
                out=std_eps[:, cols],
                in0=root[:, cols],
                scalar1=1.0 / (UNITS * math.sqrt(UNITS - 1)),
                scalar2=EPS,
                op0=ALU.mult,
                op1=ALU.add,
            )

        def inverse(std_eps, inv_std, tiles):
            cols = cols_of(tiles)
            nc.vector.reciprocal(out=inv_std[:, cols], in_=std_eps[:, cols])

        def centre(values, neg_mean, gamma, centred, tiles):
            for t in tiles:
                nc.vector.scalar_tensor_tensor(
                    out=centred[:, block(t)],
                    in0=values[:, block(t)],
                    scalar=neg_mean[:, t : t + 1],
                    in1=gamma,
                    op0=ALU.add,
                    op1=ALU.mult,
                )

        def shift(centred, std_eps, beta, tiles):
            for t in tiles:
                nc.vector.scalar_tensor_tensor(
                    out=centred[:, block(t)],
                    in0=beta,
                    scalar=std_eps[:, t : t + 1],
                    in1=centred[:, block(t)],
                    op0=ALU.mult,
                    op1=ALU.add,
                )

        ALL = range(BT)
        FIRST = range(0, BT // 2)
        LAST = range(BT // 2, BT)

        def column_tiles(what):
            return [small.tile([P, BT], F32, name="%s%d" % (what, gate)) for gate in range(GATES + 1)]

        CELL = GATES
        sums = column_tiles("sums")
        neg_means = column_tiles("neg_mean")
        sum_squares = column_tiles("sum_squares")
        roots = column_tiles("root")
        std_epss = column_tiles("std_eps")
        inv_stds = column_tiles("inv_std")
        vs = [keep.tile([P, BT * UNITS], F32, name="v%d" % gate) for gate in range(GATES)]

        def mx_product(gate, tiles):
            bank = mx_psum.tile([P, BANK], F32, tag="mx")
            for i, t in enumerate(tiles):
                for g in range(PASSES):
                    u_cols = slice(g * BATCH + t * P, g * BATCH + (t + 1) * P)
                    w_cols = slice((gate * PASSES + g) * UNITS, (gate * PASSES + g + 1) * UNITS)
                    nc.tensor.matmul_mx(
                        out=bank[:, i * UNITS : (i + 1) * UNITS],
                        lhsT=u_codes[:, u_cols].bitcast(FP8X4),
                        lhsT_scale=u_scales[:, u_cols],
                        rhs=w_codes[:, w_cols].bitcast(FP8X4),
                        rhs_scale=w_scales[:, w_cols],
                        start=(g == 0),
                        stop=(g == PASSES - 1),
                    )
            return bank

        def add_up(gate, bank, t):
            nc.vector.scalar_tensor_tensor(
                out=vs[gate][:, block(t)],
                in0=bank[:, (t % 2) * UNITS : (t % 2 + 1) * UNITS],
                scalar=1.0,
                in1=plain[:, t * N + gate * UNITS : t * N + (gate + 1) * UNITS],
                op0=ALU.mult,
                op1=ALU.add,
                accum_out=sums[gate][:, t : t + 1],
            )

        def gate_cols(gate):
            return slice(gate * UNITS, (gate + 1) * UNITS)

        def squares_of(gate, tiles):
            squares = work.tile([P, BT * UNITS], F32, tag="squares")
            sum_of_squares(vs[gate], sums[gate], squares, sum_squares[gate], tiles)


        def std_and_inverse(gate, tiles, filler=None):
            std_plus_eps(roots[gate], std_epss[gate], tiles)
            inverse(std_epss[gate], inv_stds[gate], tiles)

        normeds = {}
        gate_pool = stack.enter_context(tc.tile_pool(name="gate_pool", bufs=6))

        def normalise(gate, tiles, on_gpsimd):
            for t in tiles:
                if on_gpsimd:
                    nc.gpsimd.tensor_scalar(
                        out=normeds[gate][:, block(t)],
                        in0=vs[gate][:, block(t)],
                        scalar1=neg_means[gate][:, t : t + 1],
                        scalar2=inv_stds[gate][:, t : t + 1],
                        op0=ALU.add,
                        op1=ALU.mult,
                    )
                else:
                    nc.vector.tensor_scalar(
                        out=normeds[gate][:, block(t)],
                        in0=vs[gate][:, block(t)],
                        scalar1=neg_means[gate][:, t : t + 1],
                        scalar2=inv_stds[gate][:, t : t + 1],
                        op0=ALU.add,
                        op1=ALU.mult,
                    )

        neg_mean_over_stds = column_tiles("neg_mean_over_std")

        def mean_over_std(gate, tiles):
            cols = cols_of(tiles)
            nc.vector.tensor_tensor(
                out=neg_mean_over_stds[gate][:, cols],
                in0=neg_means[gate][:, cols],
                in1=inv_stds[gate][:, cols],
                op=ALU.mult,
            )

        def turn(gate, tiles):
            bank = flip_psum.tile([P, BANK], F32, tag="flip")
            for c in range(GATE_CHUNKS):
                for i, t in enumerate(tiles):
                    nc.tensor.transpose(
                        out=bank[:, (2 * c + i) * P : (2 * c + i + 1) * P],
                        in_=normeds[gate][:, t * UNITS + c * P : t * UNITS + (c + 1) * P],
                        identity=ident_f32[:],
                    )
            return bank

        def activate(gate, func, bank):
            gate_t = gate_pool.tile([P, BANK], F32, tag="gate_t")
            for c in range(GATE_CHUNKS):
                gamma_chunk = GAMMA_CHUNK + ORDER[gate] * GATE_CHUNKS + c
                beta_chunk = BETA_CHUNK + ORDER[gate] * GATE_CHUNKS + c
                beta = norm_cols_f32[:, beta_chunk : beta_chunk + 1]
                nc.scalar.activation(
                    out=gate_t[:, c * UNITS : (c + 1) * UNITS],
                    in_=bank[:, c * UNITS : (c + 1) * UNITS],
                    func=func,
                    scale=norm_cols_f32[:, gamma_chunk : gamma_chunk + 1],
                    bias=beta,
                )
            return gate_t

        def turn_back(gate_t, back_psum=mx_psum, back_tag="mx"):
            result = back_psum.tile([P, BANK], F32, tag=back_tag)
            for i in range(2):
                for c in range(GATE_CHUNKS):
                    first = c * UNITS + i * P
                    nc.tensor.transpose(
                        out=result[:, i * UNITS + c * P : i * UNITS + (c + 1) * P],
                        in_=gate_t[:, first : first + P],
                        identity=ident_f32[:],
                    )
            return result

        kept = keep.tile([P, BT * UNITS], F32)
        fresh = keep.tile([P, BT * UNITS], F32)
        cell = keep.tile([P, BT * UNITS], F32)
        cell_centred = keep.tile([P, BT * UNITS], F32)
        new_c = keep.tile([P, BT * UNITS], F32)
        tanh_c = keep.tile([P, BT * UNITS], F32)
        new_h = keep.tile([P, BT * UNITS], F32)
        out_0_tiles = out_0.rearrange("(p t) n -> p t n", t=BT)
        out_1_tiles = out_1.rearrange("(p t) n -> p t n", t=BT)

        def pair_cols(tiles):
            return slice(tiles.start * UNITS, tiles.stop * UNITS)

        def product(out, values, psum, tiles):
            cols = pair_cols(tiles)
            nc.vector.tensor_tensor(out=out[:, cols], in0=values[:, cols], in1=psum[:], op=ALU.mult)

        def cell_sum(tiles):
            for t in tiles:
                nc.vector.scalar_tensor_tensor(
                    out=cell[:, block(t)],
                    in0=kept[:, block(t)],
                    scalar=1.0,
                    in1=fresh[:, block(t)],
                    op0=ALU.mult,
                    op1=ALU.add,
                    accum_out=sums[CELL][:, t : t + 1],
                )

        s_copy = nc.scalar.copy
        W = {}
        U = [new_grouped() for g in range(PASSES)]

        def flip_w_half(position, i):
            W[position, i] = new_grouped()
            for b in range(2):
                flip_w(position, i, b, W[position, i], s_copy)

        def quantise_w_half(position, i):
            quantise_w(position, i, W[position, i])

        FUNC = (ACT.Sigmoid, ACT.Tanh, ACT.Sigmoid, ACT.Sigmoid)
        units = [(position, tiles) for position in range(GATES) for tiles in (FIRST, LAST)]
        for position in (0, 1, 3):
            normeds[position] = keep.tile([P, BT * UNITS], F32, name="normed%d" % position)
        centred = keep.tile([P, BT * UNITS], F32)
        gate_f = keep.tile([P, BT * UNITS], F32)
        gate_t = {}
        backs = {}

        def std_of(s):
            position, tiles = units[s]
            std_plus_eps(roots[position], std_epss[position], tiles)

        def inverse_of(s):
            position, tiles = units[s]
            inverse(std_epss[position], inv_stds[position], tiles)

        def squares_and_root(s):
            position, tiles = units[s]
            squares_of(position, tiles)
            negated_mean(sums[position], neg_means[position], tiles)
            square_root(sum_squares[position], roots[position], tiles)

        def mean_of(s):
            position, tiles = units[s]
            negated_mean(sums[position], neg_means[position], tiles)

        def normalise_of(s):
            normalise(units[s][0], units[s][1], False)

        def ratio_of(s):
            mean_over_std(units[s][0], units[s][1])

        turned = {}

        def turn_of(s):
            turned[s] = turn(units[s][0], units[s][1])

        def activate_of(s):
            gate_t[s] = activate(units[s][0], FUNC[units[s][0]], turned[s])

        def forget_centre(tiles):
            centre(vs[2], neg_means[2], gate_vector(0, 2), centred, tiles)

        def forget_shift(tiles):
            shift(centred, std_epss[2], gate_vector(1, 2), tiles)

        def forget_activate(tiles):
            for t in tiles:
                nc.scalar.activation(
                    out=gate_f[:, block(t)],
                    in_=centred[:, block(t)],
                    func=ACT.Sigmoid,
                    scale=inv_stds[2][:, t : t + 1],
                    bias=one_column[:],
                )

        def kept_half(tiles):
            cols = pair_cols(tiles)
            nc.vector.tensor_tensor(out=kept[:, cols], in0=gate_f[:, cols], in1=c_raw[:, cols], op=ALU.mult)

        def fresh_half(k):
            cols = pair_cols((FIRST, LAST)[k])
            nc.vector.tensor_tensor(out=fresh[:, cols], in0=gate_t[k][:], in1=gate_t[2 + k][:], op=ALU.mult)

        def fresh_back(k):
            cols = pair_cols((FIRST, LAST)[k])
            backs[k] = turn_back(fresh[:, cols], flip_psum, "flip")

        def cell_sum(t):
            nc.vector.scalar_tensor_tensor(
                out=cell[:, block(t)],
                in0=backs[t // 2][:, (t % 2) * UNITS : (t % 2 + 1) * UNITS],
                scalar=1.0,
                in1=kept[:, block(t)],
                op0=ALU.mult,
                op1=ALU.add,
                accum_out=sums[CELL][:, t : t + 1],
            )

        def cell_square(tiles):
            squares = work.tile([P, BT * UNITS], F32, tag="squares")
            sum_of_squares(cell, sums[CELL], squares, sum_squares[CELL], tiles)
            negated_mean(sums[CELL], neg_means[CELL], tiles)
            square_root(sum_squares[CELL], roots[CELL], tiles)

        def cell_mean(tiles):
            negated_mean(sums[CELL], neg_means[CELL], tiles)

        def cell_centre(tiles):
            centre(cell, neg_means[CELL], cell_vectors[0], cell_centred, tiles)

        def cell_std(tiles):
            std_plus_eps(roots[CELL], std_epss[CELL], tiles)

        def cell_inverse(tiles):
            inverse(std_epss[CELL], inv_stds[CELL], tiles)

        def cell_shift(tiles):
            shift(cell_centred, std_epss[CELL], cell_vectors[1], tiles)

        cell_vectors = []

        def spread_cell_vectors():
            late = flip_psum.tile([P, 2 * BANK], BF16, tag="flip")
            spread_chunks(
                late[:],
                norm_cols,
                [LNC_GAMMA_CHUNK + c for c in range(GATE_CHUNKS)] + [LNC_BETA_CHUNK + c for c in range(GATE_CHUNKS)],
            )
            cell_vectors.append(late[:, 0:UNITS])
            cell_vectors.append(late[:, UNITS : 2 * UNITS])

        def add_up_half(s, bank):
            position, tiles = units[s]
            for t in tiles:
                add_up(position, bank, t)

        def mx_half(s):
            return mx_product(units[s][0], units[s][1])

        def turn_back_of(s):
            backs[s] = turn_back(gate_t[s], plain_psum, "plain")

        def tanh_of(tiles):
            for t in tiles:
                nc.scalar.activation(
                    out=tanh_c[:, block(t)],
                    in_=cell_centred[:, block(t)],
                    func=ACT.Tanh,
                    scale=inv_stds[CELL][:, t : t + 1],
                )

        def new_c_of(tiles):
            for t in tiles:
                nc.gpsimd.tensor_scalar(
                    out=new_c[:, block(t)],
                    in0=cell_centred[:, block(t)],
                    scalar1=inv_stds[CELL][:, t : t + 1],
                    scalar2=0.0,
                    op0=ALU.mult,
                    op1=ALU.add,
                )
                nc.sync.dma_start(out=out_1_tiles[:, t, :], in_=new_c[:, block(t)])

        def output_of(tiles):
            for t in tiles:
                nc.vector.tensor_tensor(
                    out=new_h[:, block(t)],
                    in0=tanh_c[:, block(t)],
                    in1=backs[6 + t // 2][:, (t % 2) * UNITS : (t % 2 + 1) * UNITS],
                    op=ALU.mult,
                )
                nc.sync.dma_start(out=out_0_tiles[:, t, :], in_=new_h[:, block(t)])

        turn_hyper_h()
        flip_u(0, 0, U[0], s_copy)
        flip_u(1, 0, U[1], s_copy)
        turn_whh(0)
        turn_whh(1)
        turn_bias_rows()
        flip_u(0, 1, U[0], s_copy)
        flip_u(1, 1, U[1], s_copy)
        plain_first_two(0)
        quantise_u(0, U[0])
        spread_bias()
        quantise_u(1, U[1])
        for b in range(2):
            flip_u(2, b, U[2], s_copy)
            flip_u(3, b, U[3], s_copy)
        plain_first_two_out(0)
        flip_w_half(0, 0)
        quantise_u(2, U[2])
        plain_first_two(1)
        quantise_u(3, U[3])
        flip_w_half(0, 1)
        plain_first_two_out(1)
        sort(1, w_raw[1], range(2))
        quantise_w_half(0, 0)
        plain_first_two(2)
        flip_w_half(1, 0)
        quantise_w_half(0, 1)
        plain_first_two_out(2)
        flip_w_half(1, 1)
        plain_first_two(3)
        sort(2, w_raw[2], range(2))
        quantise_w_half(1, 0)

        bank_0 = mx_half(0)
        plain_first_two_out(3)
        quantise_w_half(1, 1)
        flip_w_half(2, 0)
        bank_1 = mx_half(1)
        add_up_half(0, bank_0)
        squares_and_root(0)
        flip_w_half(2, 1)
        add_up_half(1, bank_1)
        squares_and_root(1)
        quantise_w_half(2, 0)
        std_of(0)

        turn_norm_rows()
        bank_2 = mx_half(2)
        inverse_of(0)
        quantise_w_half(2, 1)
        normalise_of(0)
        bank_3 = mx_half(3)
        add_up_half(2, bank_2)
        squares_and_root(2)
        plain_one(2, FIRST)
        flip_w_half(3, 0)
        std_of(1)
        add_up_half(3, bank_3)
        inverse_of(1)
        squares_and_root(3)
        plain_one(2, LAST)
        plain_one_out(2, FIRST)
        normalise_of(1)
        std_of(2)
        plain_one_out(2, LAST)

        spread_norm_vectors()
        bank_4 = mx_half(4)
        inverse_of(2)
        quantise_w_half(3, 0)
        bank_5 = mx_half(5)
        add_up_half(4, bank_4)
        squares_and_root(4)
        normalise_of(2)
        add_up_half(5, bank_5)
        flip_w_half(3, 1)
        squares_and_root(5)
        std_of(3)
        turn_of(0)
        turn_of(2)
        forget_centre(FIRST)
        inverse_of(3)
        plain_late(3, FIRST)
        plain_late(3, LAST)
        std_of(4)
        normalise_of(3)
        turn_of(1)
        turn_of(3)
        forget_shift(FIRST)
        inverse_of(4)
        forget_centre(LAST)
        activate_of(0)
        forget_activate(FIRST)
        quantise_w_half(3, 1)
        std_of(5)
        activate_of(2)
        plain_late_out(3, FIRST)
        forget_shift(LAST)
        inverse_of(5)
        activate_of(3)
        forget_activate(LAST)
        activate_of(1)

        bank_6 = mx_half(6)
        bank_7 = mx_half(7)
        kept_half(FIRST)
        fresh_half(0)
        fresh_back(0)
        spread_cell_vectors()
        plain_late_out(3, LAST)
        add_up_half(6, bank_6)
        squares_and_root(6)
        kept_half(LAST)
        cell_sum(0)
        cell_sum(1)
        cell_square(FIRST)
        fresh_half(1)
        fresh_back(1)
        add_up_half(7, bank_7)
        std_of(6)
        inverse_of(6)
        squares_and_root(7)
        normalise_of(6)
        turn_of(6)
        cell_sum(2)
        cell_sum(3)
        cell_square(LAST)

        cell_centre(FIRST)
        cell_std(FIRST)
        activate_of(6)
        turn_back_of(6)
        std_of(7)
        cell_shift(FIRST)
        inverse_of(7)
        cell_inverse(FIRST)
        normalise_of(7)
        turn_of(7)
        tanh_of(FIRST)
        cell_centre(LAST)
        cell_std(LAST)
        activate_of(7)
        turn_back_of(7)
        new_c_of(FIRST)
        cell_shift(LAST)
        cell_inverse(LAST)
        output_of(FIRST)
        tanh_of(LAST)
        new_c_of(LAST)
        output_of(LAST)
